import numpy as np
import ml_dtypes


def mxq(x, axis, fmt="e4m3"):
    dtype, down = {"e4m3": (ml_dtypes.float8_e4m3fn, 7), "e5m2": (ml_dtypes.float8_e5m2, 14)}[fmt]
    v = np.moveaxis(np.asarray(x, np.float32).astype(ml_dtypes.bfloat16).astype(np.float64), axis, -1)
    blocks = v.reshape(v.shape[:-1] + (-1, 32))
    amax = np.abs(blocks).max(-1, keepdims=True)
    byte = np.maximum(np.where(amax > 0, np.frexp(amax)[1] - 1 + 127, 0) - down, 1)
    scale = np.exp2(byte - 127.0)
    codes = (blocks / scale).astype(np.float32).astype(dtype).astype(np.float64)
    return np.moveaxis((codes * scale).reshape(v.shape), -1, axis)


WIDE = False


def mx_kscale(k):
    if not WIDE:
        return np.ones(k)
    levels = np.array([10, -10, 5, -5, 0])
    a = np.random.permutation(np.resize(levels, k // 512 * 4)).reshape(k // 512, 4)
    idx = np.arange(k)
    return np.exp2(a[idx // 512, idx % 128 // 32])


BF16 = ml_dtypes.bfloat16


def bf(x):
    return np.asarray(x, np.float32).astype(BF16)


def f64(x):
    return np.asarray(x).astype(np.float64)


B, N, D = 16, 256, 1024


def setup_inputs():
    s = mx_kscale(D)
    return {"column_embeddings": bf(np.random.standard_normal((B, N, D)) / D**0.25 * s),
            "W": bf(np.random.uniform(-1.0, 1.0, (D, D)) * np.sqrt(3.0 / D) / s[:, None] / s[None, :]),
            "b": bf(0.3 + 0.1 * np.random.standard_normal(1))}


def reference(column_embeddings, W, b):
    xq = mxq(f64(column_embeddings), 2, "e4m3")
    xw = xq @ mxq(f64(W), 0, "e4m3")
    scores = (mxq(xw, 2, "e4m3") @ xq.transpose(0, 2, 1)) + f64(b)
    corr = np.tanh(scores)
    eye = np.eye(column_embeddings.shape[1], dtype=bool)
    return np.where(eye[None, :, :], 1.0, corr)

@@ -1,0 +1,220 @@
+from contextlib import ExitStack
+
+import concourse.mybir as mybir
+from concourse.masks import make_identity
+
+F32 = mybir.dt.float32
+BF16 = mybir.dt.bfloat16
+U32 = mybir.dt.uint32
+U8 = mybir.dt.uint8
+FP8X4 = mybir.dt.float8_e4m3fn_x4
+ACT = mybir.ActivationFunctionType
+ALU = mybir.AluOpType
+
+P = 128
+B, N, D = 16, 256, 1024
+PAIRS = B // 2
+FLOPS = 2 * B * N * D * D + 2 * B * N * N * D
+
+
+def tile_columncorrelationhead_kernel(tc, column_embeddings, W, b, out):
+    nc = tc.nc
+    x_rows = column_embeddings.flatten_outer_dims().rearrange("(c p) d -> p c d", p=P)
+    out_rows = out.flatten_outer_dims().rearrange("(c p) j -> p c j", p=P)
+    w_view = W.rearrange("(a p e) c -> p a e c", a=4, p=P, e=2)
+
+    with ExitStack() as ctx:
+        ctx.enter_context(tc.manual_schedule())
+        keep = ctx.enter_context(tc.tile_pool(name="keep", bufs=1))
+        xg_pool = ctx.enter_context(tc.tile_pool(name="xg_pool", bufs=2))
+        xwg_pool = ctx.enter_context(tc.tile_pool(name="xwg_pool", bufs=3))
+        xwc_pool = ctx.enter_context(tc.tile_pool(name="xwc_pool", bufs=4))
+        o_pool = ctx.enter_context(tc.tile_pool(name="o_pool", bufs=3))
+        tp_pool = ctx.enter_context(tc.psum_pool(name="tp_pool", bufs=4))
+        mm_pool = ctx.enter_context(tc.psum_pool(name="mm_pool", bufs=4))
+
+        def copy(engine, dst, src):
+            if engine == "v":
+                nc.vector.tensor_copy(out=dst, in_=src)
+            else:
+                nc.scalar.copy(out=dst, in_=src)
+
+        ident = keep.tile([P, P], F32, name="ident")
+        make_identity(nc, ident[:])
+        mask = keep.tile([P, P], F32, name="mask")
+        nc.vector.tensor_scalar(out=mask[:], in0=ident[:], scalar1=2.0, scalar2=-1.0,
+                                op0=ALU.mult, op1=ALU.add)
+        b_bf = keep.tile([P, 1], BF16, name="b_bf")
+        nc.scalar.dma_start(out=b_bf[:], in_=b.partition_broadcast(P))
+        warm = keep.tile([P, 1], F32, name="warm")
+        nc.scalar.activation(out=warm[:], in_=ident[:, 0:1], func=ACT.Tanh)
+        bias = keep.tile([P, 1], F32, name="bias")
+
+        xraw = [keep.tile([P, 4, D], BF16, name="xraw%d" % q) for q in range(PAIRS)]
+        wraw = [keep.tile([P, 4, 2, 512], BF16, name="wraw%d" % h) for h in range(2)]
+        nc.sync.dma_start(out=xraw[0][:, 0:2, :], in_=x_rows[:, 0:2, :])
+        nc.sync.dma_start(out=xraw[0][:, 2:4, :], in_=x_rows[:, 2:4, :])
+        for h in range(2):
+            for e in range(2):
+                nc.sync.dma_start(out=wraw[h][:, :, e, :],
+                                  in_=w_view[:, :, e, h * 512:(h + 1) * 512])
+        for q in range(1, PAIRS):
+            nc.sync.dma_start(out=xraw[q][:], in_=x_rows[:, 4 * q:4 * q + 4, :])
+
+        xc = [keep.tile([P, 2, 2, N], U32, name="xc%d" % q, align_bytes=64) for q in range(PAIRS)]
+        xs = [keep.tile([P, 2, 2, N], U8, name="xs%d" % q, align_bytes=64) for q in range(PAIRS)]
+        wg = [keep.tile([P, 2, 2048], BF16, name="wg%d" % h, align_bytes=64) for h in range(2)]
+        wc = [keep.tile([P, 2, 512], U32, name="wc%d" % h, align_bytes=64) for h in range(2)]
+        ws = [keep.tile([P, 2, 512], U8, name="ws%d" % h, align_bytes=64) for h in range(2)]
+
+        state = {}
+
+        def transposes(q):
+            x32 = xraw[q][:].bitcast(F32)
+            banks = []
+            for n2 in range(2):
+                for g in range(2):
+                    tp = tp_pool.tile([P, 2, N], F32, name="tp", tag="tp")
+                    for u in range(2):
+                        for rb in range(2):
+                            lo = 256 * g + 128 * u
+                            nc.tensor.transpose(tp[:, u, rb * P:(rb + 1) * P],
+                                                x32[:, 2 * n2 + rb, lo:lo + P], ident[:])
+                    banks.append(tp)
+            state["tp"] = banks
+            state["xg"] = xg_pool.tile([P, 2, 2, 4 * N], BF16, name="xg", tag="xg", align_bytes=64)
+
+        def t_copy(k, engine):
+            n2, g = divmod(k, 2)
+            xg32 = state["xg"][:].bitcast(F32)
+            copy(engine, xg32[:, n2, g, :].rearrange("p (i u) -> p i u", u=2),
+                 state["tp"][k][:].rearrange("p u i -> p i u"))
+
+        def quant_x(q, n2):
+            nc.vector.quantize_mx(
+                out=xc[q][:, n2].rearrange("p g i -> p (g i)").bitcast(FP8X4),
+                scales=xs[q][:, n2].rearrange("p g i -> p (g i)"),
+                in_=state["xg"][:, n2].rearrange("p g c -> p (g c)"))
+
+        def w_regroup(h, gd, v, f, engine):
+            src = wraw[h][:].rearrange("p a e c -> p (a e) c")[:, 4 * gd:4 * gd + 4, :]
+            src = src.rearrange("p t (v q f) -> p v f q t", v=2, q=P, f=2)[:, v, f]
+            dst = wg[h][:, gd, :].rearrange("p (v f q t) -> p v f q t", v=2, f=2, q=P, t=4)[:, v, f]
+            copy(engine, dst, src)
+
+        def w_quant(h, gd):
+            nc.vector.quantize_mx(out=wc[h][:, gd, :].bitcast(FP8X4), scales=ws[h][:, gd, :],
+                                  in_=wg[h][:, gd, :])
+
+        def w_prep(h):
+            w_regroup(h, 0, 0, 0, "v")
+            w_regroup(h, 0, 0, 1, "v")
+            w_regroup(h, 0, 1, 0, "v")
+            w_regroup(h, 0, 1, 1, "s")
+            w_regroup(h, 1, 0, 0, "v")
+            w_regroup(h, 1, 0, 1, "s")
+            w_regroup(h, 1, 1, 0, "v")
+            w_regroup(h, 1, 1, 1, "s")
+            w_quant(h, 0)
+            w_quant(h, 1)
+
+        def first_matmul(q, ge, cb, engine):
+            if cb == 0:
+                state["xwg"] = xwg_pool.tile([P, 512, 4], BF16, name="xwg", tag="xwg", align_bytes=64)
+            n2, ib = divmod(cb, 2)
+            mm = mm_pool.tile([P, 512], F32, name="mm", tag="mm")
+            cols = slice(ib * P, (ib + 1) * P)
+            for t in range(4):
+                blk = slice(t * P, (t + 1) * P)
+                for gd in range(2):
+                    nc.tensor.matmul_mx(out=mm[:, blk],
+                                        lhsT=wc[ge][:, gd, blk].bitcast(FP8X4),
+                                        lhsT_scale=ws[ge][:, gd, blk],
+                                        rhs=xc[q][:, n2, gd, cols].bitcast(FP8X4),
+                                        rhs_scale=xs[q][:, n2, gd, cols],
+                                        start=(gd == 0), stop=(gd == 1))
+            copy(engine, state["xwg"][:, cb * P:(cb + 1) * P, :],
+                 mm[:].rearrange("p (t i) -> p i t", t=4))
+
+        def quant_xw(q, ge):
+            codes = xwc_pool.tile([P, 512], U32, name="xwc", tag="xwc", align_bytes=64)
+            planes = xwc_pool.tile([P, 512], U8, name="xws", tag="xws", align_bytes=64)
+            nc.vector.quantize_mx(out=codes[:].bitcast(FP8X4), scales=planes[:],
+                                  in_=state["xwg"][:].rearrange("p i t -> p (i t)"))
+            state[("xwc", q, ge)] = (codes, planes)
+
+        def second_matmul(q, n2):
+            if n2 == 0:
+                state[("o", q)] = o_pool.tile([P, 4, N], F32, name="o", tag="o")
+            mm = mm_pool.tile([P, 512], F32, name="mm", tag="mm")
+            for ib in range(2):
+                blk = slice((2 * n2 + ib) * P, (2 * n2 + ib + 1) * P)
+                for ge in range(2):
+                    codes, planes = state[("xwc", q, ge)]
+                    nc.tensor.matmul_mx(out=mm[:, ib * N:(ib + 1) * N],
+                                        lhsT=codes[:, blk].bitcast(FP8X4),
+                                        lhsT_scale=planes[:, blk],
+                                        rhs=xc[q][:, n2, ge, :].bitcast(FP8X4),
+                                        rhs_scale=xs[q][:, n2, ge, :],
+                                        start=(ge == 0), stop=(ge == 1))
+            nc.scalar.activation(out=state[("o", q)][:, 2 * n2:2 * n2 + 2, :],
+                                 in_=mm[:].rearrange("p (r j) -> p r j", r=2),
+                                 func=ACT.Tanh, bias=bias[:, 0:1], scale=1.0)
+
+        def finish(q, n_lo, n_hi):
+            o = state[("o", q)]
+            diag = o[:, 2 * n_lo:2 * n_hi, :].rearrange("p (n r) (a k) -> p n (r a) k", r=2, k=P)
+            diag = diag[:, :, 0:4:3, :]
+            nc.vector.tensor_tensor(
+                out=diag, in0=diag,
+                in1=mask[:].unsqueeze(1).unsqueeze(1).to_broadcast([P, n_hi - n_lo, 2, P]),
+                op=ALU.max)
+            nc.sync.dma_start(out=out_rows[:, 4 * q + 2 * n_lo:4 * q + 2 * n_hi, :],
+                              in_=o[:, 2 * n_lo:2 * n_hi, :])
+
+        transposes(0)
+        t_copy(0, "v")
+        t_copy(1, "s")
+        t_copy(2, "v")
+        t_copy(3, "s")
+        quant_x(0, 0)
+        quant_x(0, 1)
+        w_prep(0)
+        nc.vector.tensor_copy(out=bias[:], in_=b_bf[:])
+
+        for q in range(PAIRS):
+            first_matmul(q, 0, 0, "s")
+            first_matmul(q, 0, 1, "s")
+            if q == 0:
+                w_prep(1)
+            if q >= 2:
+                finish(q - 2, 0, 2)
+            first_matmul(q, 0, 2, "v")
+            first_matmul(q, 0, 3, "s")
+            more = q + 1 < PAIRS
+            if more:
+                transposes(q + 1)
+                t_copy(0, "v")
+            quant_xw(q, 0)
+            if more:
+                t_copy(1, "v")
+                t_copy(2, "v")
+                t_copy(3, "s")
+            first_matmul(q, 1, 0, "s")
+            if more:
+                quant_x(q + 1, 0)
+            first_matmul(q, 1, 1, "s")
+            first_matmul(q, 1, 2, "v")
+            if more:
+                quant_x(q + 1, 1)
+            first_matmul(q, 1, 3, "s")
+            quant_xw(q, 1)
+            if q >= 1:
+                second_matmul(q - 1, 0)
+                second_matmul(q - 1, 1)
+
+        finish(PAIRS - 2, 0, 2)
+        second_matmul(PAIRS - 1, 0)
+        finish(PAIRS - 1, 0, 1)
+        second_matmul(PAIRS - 1, 1)
+        finish(PAIRS - 1, 1, 2)

@@ -24,7 +24,6 @@ def tile_columncorrelationhead_kernel(tc, column_embeddings, W, b, out):
     w_view = W.rearrange("(a p e) c -> p a e c", a=4, p=P, e=2)
 
     with ExitStack() as ctx:
-        ctx.enter_context(tc.manual_schedule())
         keep = ctx.enter_context(tc.tile_pool(name="keep", bufs=1))
         xg_pool = ctx.enter_context(tc.tile_pool(name="xg_pool", bufs=2))
         xwg_pool = ctx.enter_context(tc.tile_pool(name="xwg_pool", bufs=3))

@@ -13,8 +13,8 @@ ALU = mybir.AluOpType
 
 P = 128
 B, N, D = 16, 256, 1024
-PAIRS = B // 2
 FLOPS = 2 * B * N * D * D + 2 * B * N * N * D
+SOLO = ((14, 1), (15, 1))
 
 
 def tile_columncorrelationhead_kernel(tc, column_embeddings, W, b, out):
@@ -24,11 +24,13 @@ def tile_columncorrelationhead_kernel(tc, column_embeddings, W, b, out):
     w_view = W.rearrange("(a p e) c -> p a e c", a=4, p=P, e=2)
 
     with ExitStack() as ctx:
+        ctx.enter_context(tc.manual_schedule())
         keep = ctx.enter_context(tc.tile_pool(name="keep", bufs=1))
-        xg_pool = ctx.enter_context(tc.tile_pool(name="xg_pool", bufs=2))
-        xwg_pool = ctx.enter_context(tc.tile_pool(name="xwg_pool", bufs=3))
-        xwc_pool = ctx.enter_context(tc.tile_pool(name="xwc_pool", bufs=4))
-        o_pool = ctx.enter_context(tc.tile_pool(name="o_pool", bufs=3))
+        xg_pool = ctx.enter_context(tc.tile_pool(name="xg_pool", bufs=4))
+        xwg_pool = ctx.enter_context(tc.tile_pool(name="xwg_pool", bufs=5))
+        xwc_pool = ctx.enter_context(tc.tile_pool(name="xwc_pool", bufs=6))
+        solo_pool = ctx.enter_context(tc.tile_pool(name="solo_pool", bufs=2))
+        o_pool = ctx.enter_context(tc.tile_pool(name="o_pool", bufs=6))
         tp_pool = ctx.enter_context(tc.psum_pool(name="tp_pool", bufs=4))
         mm_pool = ctx.enter_context(tc.psum_pool(name="mm_pool", bufs=4))
 
@@ -49,171 +51,341 @@ def tile_columncorrelationhead_kernel(tc, column_embeddings, W, b, out):
         nc.scalar.activation(out=warm[:], in_=ident[:, 0:1], func=ACT.Tanh)
         bias = keep.tile([P, 1], F32, name="bias")
 
-        xraw = [keep.tile([P, 4, D], BF16, name="xraw%d" % q) for q in range(PAIRS)]
-        wraw = [keep.tile([P, 4, 2, 512], BF16, name="wraw%d" % h) for h in range(2)]
-        nc.sync.dma_start(out=xraw[0][:, 0:2, :], in_=x_rows[:, 0:2, :])
-        nc.sync.dma_start(out=xraw[0][:, 2:4, :], in_=x_rows[:, 2:4, :])
-        for h in range(2):
-            for e in range(2):
-                nc.sync.dma_start(out=wraw[h][:, :, e, :],
-                                  in_=w_view[:, :, e, h * 512:(h + 1) * 512])
-        for q in range(1, PAIRS):
-            nc.sync.dma_start(out=xraw[q][:], in_=x_rows[:, 4 * q:4 * q + 4, :])
-
-        xc = [keep.tile([P, 2, 2, N], U32, name="xc%d" % q, align_bytes=64) for q in range(PAIRS)]
-        xs = [keep.tile([P, 2, 2, N], U8, name="xs%d" % q, align_bytes=64) for q in range(PAIRS)]
-        wg = [keep.tile([P, 2, 2048], BF16, name="wg%d" % h, align_bytes=64) for h in range(2)]
-        wc = [keep.tile([P, 2, 512], U32, name="wc%d" % h, align_bytes=64) for h in range(2)]
-        ws = [keep.tile([P, 2, 512], U8, name="ws%d" % h, align_bytes=64) for h in range(2)]
-
+        xraw = [keep.tile([P, 2, D], BF16, name="xraw%d" % n) for n in range(B)]
+        xc = [keep.tile([P, 2, N], U32, name="xc%d" % n, align_bytes=64) for n in range(B)]
+        xs = [keep.tile([P, 2, N], U8, name="xs%d" % n, align_bytes=64) for n in range(B)]
+        wraw = [[keep.tile([P, 2, 2, 512], BF16, name="wraw%d%d" % (h, gd)) for gd in range(2)]
+                for h in range(2)]
+        wg = [[keep.tile([P, 2048], BF16, name="wg%d%d" % (h, gd), align_bytes=64) for gd in range(2)]
+              for h in range(2)]
+        wc = [[keep.tile([P, 512], U32, name="wc%d%d" % (h, gd), align_bytes=64) for gd in range(2)]
+              for h in range(2)]
+        ws = [[keep.tile([P, 512], U8, name="ws%d%d" % (h, gd), align_bytes=64) for gd in range(2)]
+              for h in range(2)]
         state = {}
 
-        def transposes(q):
-            x32 = xraw[q][:].bitcast(F32)
-            banks = []
-            for n2 in range(2):
-                for g in range(2):
-                    tp = tp_pool.tile([P, 2, N], F32, name="tp", tag="tp")
-                    for u in range(2):
-                        for rb in range(2):
-                            lo = 256 * g + 128 * u
-                            nc.tensor.transpose(tp[:, u, rb * P:(rb + 1) * P],
-                                                x32[:, 2 * n2 + rb, lo:lo + P], ident[:])
-                    banks.append(tp)
-            state["tp"] = banks
-            state["xg"] = xg_pool.tile([P, 2, 2, 4 * N], BF16, name="xg", tag="xg", align_bytes=64)
+        def load_x(n):
+            nc.sync.dma_start(out=xraw[n][:], in_=x_rows[:, 2 * n:2 * n + 2, :])
 
-        def t_copy(k, engine):
-            n2, g = divmod(k, 2)
-            xg32 = state["xg"][:].bitcast(F32)
-            copy(engine, xg32[:, n2, g, :].rearrange("p (i u) -> p i u", u=2),
-                 state["tp"][k][:].rearrange("p u i -> p i u"))
+        def load_w(h, gd):
+            for e in range(2):
+                nc.sync.dma_start(out=wraw[h][gd][:, :, e, :],
+                                  in_=w_view[:, 2 * gd:2 * gd + 2, e, h * 512:(h + 1) * 512])
 
-        def quant_x(q, n2):
-            nc.vector.quantize_mx(
-                out=xc[q][:, n2].rearrange("p g i -> p (g i)").bitcast(FP8X4),
-                scales=xs[q][:, n2].rearrange("p g i -> p (g i)"),
-                in_=state["xg"][:, n2].rearrange("p g c -> p (g c)"))
+        def transposes(n):
+            x32 = xraw[n][:].bitcast(F32)
+            for g in range(2):
+                tp = tp_pool.tile([P, 2, N], F32, name="tp", tag="tp")
+                for u in range(2):
+                    for rb in range(2):
+                        lo = 256 * g + 128 * u
+                        nc.tensor.transpose(tp[:, u, rb * P:(rb + 1) * P],
+                                            x32[:, rb, lo:lo + P], ident[:])
+                state[("tp", n, g)] = tp
+            state[("xg", n)] = xg_pool.tile([P, 2, 4 * N], BF16, name="xg", tag="xg", align_bytes=64)
 
-        def w_regroup(h, gd, v, f, engine):
-            src = wraw[h][:].rearrange("p a e c -> p (a e) c")[:, 4 * gd:4 * gd + 4, :]
+        def t_copy(n, g, engine):
+            xg32 = state[("xg", n)][:].bitcast(F32)
+            copy(engine, xg32[:, g, :].rearrange("p (i u) -> p i u", u=2),
+                 state[("tp", n, g)][:].rearrange("p u i -> p i u"))
+
+        def quant_x(n):
+            nc.vector.quantize_mx(out=xc[n][:].rearrange("p g i -> p (g i)").bitcast(FP8X4),
+                                  scales=xs[n][:].rearrange("p g i -> p (g i)"),
+                                  in_=state[("xg", n)][:].rearrange("p g c -> p (g c)"))
+
+        def w_regroup(h, gd, piece, engine):
+            v, f = divmod(piece, 2)
+            src = wraw[h][gd][:].rearrange("p u e c -> p (u e) c")
             src = src.rearrange("p t (v q f) -> p v f q t", v=2, q=P, f=2)[:, v, f]
-            dst = wg[h][:, gd, :].rearrange("p (v f q t) -> p v f q t", v=2, f=2, q=P, t=4)[:, v, f]
+            dst = wg[h][gd][:].rearrange("p (v f q t) -> p v f q t", v=2, f=2, q=P, t=4)[:, v, f]
             copy(engine, dst, src)
 
         def w_quant(h, gd):
-            nc.vector.quantize_mx(out=wc[h][:, gd, :].bitcast(FP8X4), scales=ws[h][:, gd, :],
-                                  in_=wg[h][:, gd, :])
+            nc.vector.quantize_mx(out=wc[h][gd][:].bitcast(FP8X4), scales=ws[h][gd][:],
+                                  in_=wg[h][gd][:])
 
-        def w_prep(h):
-            w_regroup(h, 0, 0, 0, "v")
-            w_regroup(h, 0, 0, 1, "v")
-            w_regroup(h, 0, 1, 0, "v")
-            w_regroup(h, 0, 1, 1, "s")
-            w_regroup(h, 1, 0, 0, "v")
-            w_regroup(h, 1, 0, 1, "s")
-            w_regroup(h, 1, 1, 0, "v")
-            w_regroup(h, 1, 1, 1, "s")
-            w_quant(h, 0)
-            w_quant(h, 1)
+        def xw_place(n, ge):
+            if (n, ge) in SOLO:
+                return (n, ge), 0, 1
+            return (n - n % 2, ge), n % 2, 2
 
-        def first_matmul(q, ge, cb, engine):
-            if cb == 0:
-                state["xwg"] = xwg_pool.tile([P, 512, 4], BF16, name="xwg", tag="xwg", align_bytes=64)
-            n2, ib = divmod(cb, 2)
+        def first_matmul(n, ge, ib, engine):
+            key, half, width = xw_place(n, ge)
+            if ("xwg", key) not in state:
+                if width == 1:
+                    state[("xwg", key)] = solo_pool.tile([P, N, 4], BF16, name="xwg1", tag="xwg1",
+                                                         align_bytes=64)
+                else:
+                    state[("xwg", key)] = xwg_pool.tile([P, 2 * N, 4], BF16, name="xwg", tag="xwg",
+                                                        align_bytes=64)
             mm = mm_pool.tile([P, 512], F32, name="mm", tag="mm")
             cols = slice(ib * P, (ib + 1) * P)
             for t in range(4):
                 blk = slice(t * P, (t + 1) * P)
                 for gd in range(2):
                     nc.tensor.matmul_mx(out=mm[:, blk],
-                                        lhsT=wc[ge][:, gd, blk].bitcast(FP8X4),
-                                        lhsT_scale=ws[ge][:, gd, blk],
-                                        rhs=xc[q][:, n2, gd, cols].bitcast(FP8X4),
-                                        rhs_scale=xs[q][:, n2, gd, cols],
+                                        lhsT=wc[ge][gd][:, blk].bitcast(FP8X4),
+                                        lhsT_scale=ws[ge][gd][:, blk],
+                                        rhs=xc[n][:, gd, cols].bitcast(FP8X4),
+                                        rhs_scale=xs[n][:, gd, cols],
                                         start=(gd == 0), stop=(gd == 1))
-            copy(engine, state["xwg"][:, cb * P:(cb + 1) * P, :],
+            lo = (2 * half + ib) * P
+            copy(engine, state[("xwg", key)][:, lo:lo + P, :],
                  mm[:].rearrange("p (t i) -> p i t", t=4))
 
-        def quant_xw(q, ge):
-            codes = xwc_pool.tile([P, 512], U32, name="xwc", tag="xwc", align_bytes=64)
-            planes = xwc_pool.tile([P, 512], U8, name="xws", tag="xws", align_bytes=64)
+        def quant_xw(n, ge, width):
+            key = xw_place(n, ge)[0]
+            if width == 1:
+                codes = solo_pool.tile([P, N], U32, name="xwc1", tag="xwc1", align_bytes=64)
+                planes = solo_pool.tile([P, N], U8, name="xws1", tag="xws1", align_bytes=64)
+            else:
+                codes = xwc_pool.tile([P, 2 * N], U32, name="xwc", tag="xwc", align_bytes=64)
+                planes = xwc_pool.tile([P, 2 * N], U8, name="xws", tag="xws", align_bytes=64)
             nc.vector.quantize_mx(out=codes[:].bitcast(FP8X4), scales=planes[:],
-                                  in_=state["xwg"][:].rearrange("p i t -> p (i t)"))
-            state[("xwc", q, ge)] = (codes, planes)
+                                  in_=state[("xwg", key)][:].rearrange("p i t -> p (i t)"))
+            state[("xwc", key)] = (codes, planes)
 
-        def second_matmul(q, n2):
-            if n2 == 0:
-                state[("o", q)] = o_pool.tile([P, 4, N], F32, name="o", tag="o")
+        def second_matmul(n):
+            o = o_pool.tile([P, 2, N], F32, name="o", tag="o")
+            state[("o", n)] = o
             mm = mm_pool.tile([P, 512], F32, name="mm", tag="mm")
             for ib in range(2):
-                blk = slice((2 * n2 + ib) * P, (2 * n2 + ib + 1) * P)
                 for ge in range(2):
-                    codes, planes = state[("xwc", q, ge)]
+                    key, half, width = xw_place(n, ge)
+                    codes, planes = state[("xwc", key)]
+                    blk = slice((2 * half + ib) * P, (2 * half + ib + 1) * P)
                     nc.tensor.matmul_mx(out=mm[:, ib * N:(ib + 1) * N],
                                         lhsT=codes[:, blk].bitcast(FP8X4),
                                         lhsT_scale=planes[:, blk],
-                                        rhs=xc[q][:, n2, ge, :].bitcast(FP8X4),
-                                        rhs_scale=xs[q][:, n2, ge, :],
+                                        rhs=xc[n][:, ge, :].bitcast(FP8X4),
+                                        rhs_scale=xs[n][:, ge, :],
                                         start=(ge == 0), stop=(ge == 1))
-            nc.scalar.activation(out=state[("o", q)][:, 2 * n2:2 * n2 + 2, :],
-                                 in_=mm[:].rearrange("p (r j) -> p r j", r=2),
+            nc.scalar.activation(out=o[:], in_=mm[:].rearrange("p (r j) -> p r j", r=2),
                                  func=ACT.Tanh, bias=bias[:, 0:1], scale=1.0)
 
-        def finish(q, n_lo, n_hi):
-            o = state[("o", q)]
-            diag = o[:, 2 * n_lo:2 * n_hi, :].rearrange("p (n r) (a k) -> p n (r a) k", r=2, k=P)
-            diag = diag[:, :, 0:4:3, :]
-            nc.vector.tensor_tensor(
-                out=diag, in0=diag,
-                in1=mask[:].unsqueeze(1).unsqueeze(1).to_broadcast([P, n_hi - n_lo, 2, P]),
-                op=ALU.max)
-            nc.sync.dma_start(out=out_rows[:, 4 * q + 2 * n_lo:4 * q + 2 * n_hi, :],
-                              in_=o[:, 2 * n_lo:2 * n_hi, :])
+        def finish(n):
+            o = state[("o", n)]
+            diag = o[:].rearrange("p r (a k) -> p (r a) k", k=P)[:, 0:4:3, :]
+            nc.vector.tensor_tensor(out=diag, in0=diag,
+                                    in1=mask[:].unsqueeze(1).to_broadcast([P, 2, P]), op=ALU.max)
+            nc.sync.dma_start(out=out_rows[:, 2 * n:2 * n + 2, :], in_=o[:])
 
+        load_x(0)
+        load_w(0, 0)
+        load_w(0, 1)
+        load_x(1)
+        load_x(2)
+        load_x(3)
+        load_x(4)
+        load_x(5)
+        load_w(1, 0)
+        load_w(1, 1)
+        load_x(6)
+        load_x(7)
+        load_x(8)
+        load_x(9)
+        load_x(10)
+        load_x(11)
+        load_x(12)
+        load_x(13)
+        load_x(14)
+        load_x(15)
         transposes(0)
-        t_copy(0, "v")
-        t_copy(1, "s")
-        t_copy(2, "v")
-        t_copy(3, "s")
-        quant_x(0, 0)
-        quant_x(0, 1)
-        w_prep(0)
+        t_copy(0, 0, "s")
+        t_copy(0, 1, "v")
+        w_regroup(0, 0, 0, "s")
+        quant_x(0)
+        w_regroup(0, 0, 1, "s")
+        w_regroup(0, 0, 2, "v")
+        w_regroup(0, 0, 3, "v")
+        w_quant(0, 0)
+        w_regroup(0, 1, 0, "s")
+        w_regroup(0, 1, 1, "v")
+        w_regroup(0, 1, 2, "s")
+        w_regroup(0, 1, 3, "v")
+        w_quant(0, 1)
         nc.vector.tensor_copy(out=bias[:], in_=b_bf[:])
-
-        for q in range(PAIRS):
-            first_matmul(q, 0, 0, "s")
-            first_matmul(q, 0, 1, "s")
-            if q == 0:
-                w_prep(1)
-            if q >= 2:
-                finish(q - 2, 0, 2)
-            first_matmul(q, 0, 2, "v")
-            first_matmul(q, 0, 3, "s")
-            more = q + 1 < PAIRS
-            if more:
-                transposes(q + 1)
-                t_copy(0, "v")
-            quant_xw(q, 0)
-            if more:
-                t_copy(1, "v")
-                t_copy(2, "v")
-                t_copy(3, "s")
-            first_matmul(q, 1, 0, "s")
-            if more:
-                quant_x(q + 1, 0)
-            first_matmul(q, 1, 1, "s")
-            first_matmul(q, 1, 2, "v")
-            if more:
-                quant_x(q + 1, 1)
-            first_matmul(q, 1, 3, "s")
-            quant_xw(q, 1)
-            if q >= 1:
-                second_matmul(q - 1, 0)
-                second_matmul(q - 1, 1)
-
-        finish(PAIRS - 2, 0, 2)
-        second_matmul(PAIRS - 1, 0)
-        finish(PAIRS - 1, 0, 1)
-        second_matmul(PAIRS - 1, 1)
-        finish(PAIRS - 1, 1, 2)
+        transposes(1)
+        t_copy(1, 0, "s")
+        t_copy(1, 1, "v")
+        quant_x(1)
+        first_matmul(0, 0, 0, "s")
+        first_matmul(0, 0, 1, "v")
+        transposes(2)
+        transposes(3)
+        t_copy(2, 0, "s")
+        t_copy(2, 1, "v")
+        t_copy(3, 0, "s")
+        t_copy(3, 1, "v")
+        quant_x(2)
+        first_matmul(1, 0, 0, "s")
+        quant_x(3)
+        first_matmul(1, 0, 1, "s")
+        first_matmul(2, 0, 0, "v")
+        first_matmul(2, 0, 1, "s")
+        transposes(4)
+        transposes(5)
+        t_copy(4, 0, "v")
+        t_copy(4, 1, "s")
+        t_copy(5, 0, "v")
+        t_copy(5, 1, "s")
+        quant_x(4)
+        first_matmul(3, 0, 0, "s")
+        quant_x(5)
+        first_matmul(3, 0, 1, "s")
+        w_regroup(1, 0, 0, "v")
+        w_regroup(1, 0, 1, "v")
+        first_matmul(4, 0, 0, "s")
+        w_regroup(1, 0, 2, "v")
+        w_regroup(1, 0, 3, "v")
+        first_matmul(4, 0, 1, "s")
+        w_quant(1, 0)
+        w_regroup(1, 1, 0, "v")
+        first_matmul(5, 0, 0, "s")
+        w_regroup(1, 1, 1, "v")
+        w_regroup(1, 1, 2, "v")
+        first_matmul(5, 0, 1, "s")
+        w_regroup(1, 1, 3, "v")
+        w_quant(1, 1)
+        transposes(6)
+        transposes(7)
+        t_copy(6, 0, "s")
+        t_copy(6, 1, "s")
+        t_copy(7, 0, "s")
+        t_copy(7, 1, "s")
+        quant_xw(0, 0, 2)
+        first_matmul(0, 1, 0, "v")
+        quant_xw(2, 0, 2)
+        first_matmul(0, 1, 1, "s")
+        quant_xw(4, 0, 2)
+        first_matmul(1, 1, 0, "s")
+        quant_x(6)
+        first_matmul(1, 1, 1, "s")
+        quant_x(7)
+        first_matmul(2, 1, 0, "s")
+        quant_xw(0, 1, 2)
+        first_matmul(2, 1, 1, "v")
+        first_matmul(3, 1, 0, "s")
+        first_matmul(3, 1, 1, "s")
+        second_matmul(0)
+        quant_xw(2, 1, 2)
+        second_matmul(1)
+        first_matmul(4, 1, 0, "s")
+        finish(0)
+        first_matmul(4, 1, 1, "s")
+        finish(1)
+        first_matmul(5, 1, 0, "v")
+        first_matmul(5, 1, 1, "s")
+        quant_xw(4, 1, 2)
+        second_matmul(2)
+        second_matmul(3)
+        first_matmul(6, 0, 0, "s")
+        first_matmul(6, 0, 1, "s")
+        finish(2)
+        finish(3)
+        first_matmul(7, 0, 0, "v")
+        first_matmul(7, 0, 1, "s")
+        second_matmul(4)
+        quant_xw(6, 0, 2)
+        second_matmul(5)
+        transposes(8)
+        transposes(9)
+        t_copy(8, 0, "v")
+        t_copy(8, 1, "v")
+        t_copy(9, 0, "s")
+        t_copy(9, 1, "v")
+        first_matmul(6, 1, 0, "s")
+        quant_x(8)
+        first_matmul(6, 1, 1, "s")
+        first_matmul(7, 1, 0, "v")
+        quant_x(9)
+        first_matmul(7, 1, 1, "s")
+        quant_xw(6, 1, 2)
+        first_matmul(8, 0, 0, "s")
+        first_matmul(8, 0, 1, "s")
+        finish(4)
+        finish(5)
+        first_matmul(9, 0, 0, "v")
+        first_matmul(9, 0, 1, "s")
+        second_matmul(6)
+        quant_xw(8, 0, 2)
+        second_matmul(7)
+        transposes(10)
+        transposes(11)
+        t_copy(10, 0, "v")
+        t_copy(10, 1, "v")
+        t_copy(11, 0, "s")
+        t_copy(11, 1, "v")
+        first_matmul(8, 1, 0, "s")
+        quant_x(10)
+        first_matmul(8, 1, 1, "s")
+        first_matmul(9, 1, 0, "v")
+        quant_x(11)
+        first_matmul(9, 1, 1, "s")
+        quant_xw(8, 1, 2)
+        first_matmul(10, 0, 0, "s")
+        first_matmul(10, 0, 1, "s")
+        finish(6)
+        finish(7)
+        first_matmul(11, 0, 0, "v")
+        first_matmul(11, 0, 1, "s")
+        second_matmul(8)
+        quant_xw(10, 0, 2)
+        second_matmul(9)
+        transposes(12)
+        transposes(13)
+        t_copy(12, 0, "v")
+        t_copy(12, 1, "v")
+        t_copy(13, 0, "s")
+        t_copy(13, 1, "v")
+        first_matmul(10, 1, 0, "s")
+        quant_x(12)
+        first_matmul(10, 1, 1, "s")
+        first_matmul(11, 1, 0, "v")
+        quant_x(13)
+        first_matmul(11, 1, 1, "s")
+        quant_xw(10, 1, 2)
+        first_matmul(12, 0, 0, "s")
+        first_matmul(12, 0, 1, "s")
+        finish(8)
+        finish(9)
+        first_matmul(13, 0, 0, "v")
+        first_matmul(13, 0, 1, "s")
+        second_matmul(10)
+        quant_xw(12, 0, 2)
+        second_matmul(11)
+        transposes(14)
+        transposes(15)
+        t_copy(14, 0, "v")
+        t_copy(14, 1, "v")
+        t_copy(15, 0, "s")
+        t_copy(15, 1, "v")
+        first_matmul(12, 1, 0, "s")
+        quant_x(14)
+        first_matmul(12, 1, 1, "s")
+        first_matmul(13, 1, 0, "v")
+        quant_x(15)
+        first_matmul(13, 1, 1, "s")
+        quant_xw(12, 1, 2)
+        first_matmul(14, 0, 0, "s")
+        first_matmul(14, 0, 1, "s")
+        finish(10)
+        finish(11)
+        first_matmul(15, 0, 0, "v")
+        first_matmul(15, 0, 1, "s")
+        quant_xw(14, 0, 2)
+        first_matmul(14, 1, 0, "s")
+        first_matmul(14, 1, 1, "v")
+        first_matmul(15, 1, 0, "s")
+        quant_xw(14, 1, 1)
+        first_matmul(15, 1, 1, "v")
+        second_matmul(12)
+        quant_xw(15, 1, 1)
+        second_matmul(13)
+        second_matmul(14)
+        finish(12)
+        second_matmul(15)
+        finish(13)
+        finish(14)
+        finish(15)

@@ -7,6 +7,7 @@ F32 = mybir.dt.float32
 BF16 = mybir.dt.bfloat16
 U32 = mybir.dt.uint32
 U8 = mybir.dt.uint8
+I32 = mybir.dt.int32
 FP8X4 = mybir.dt.float8_e4m3fn_x4
 ACT = mybir.ActivationFunctionType
 ALU = mybir.AluOpType
@@ -40,6 +41,11 @@ def tile_columncorrelationhead_kernel(tc, column_embeddings, W, b, out):
             else:
                 nc.scalar.copy(out=dst, in_=src)
 
+        zero_codes = keep.tile([P, 512], U32, name="zero_codes", align_bytes=64)
+        zero_scales = keep.tile([P, 512], U8, name="zero_scales", align_bytes=64)
+        zeros = keep.tile([P, 2048], BF16, name="zeros", align_bytes=64)
+        nc.vector.memset(zeros[:].bitcast(I32), 0)
+        nc.vector.quantize_mx(out=zero_codes[:].bitcast(FP8X4), scales=zero_scales[:], in_=zeros[:])
         ident = keep.tile([P, P], F32, name="ident")
         make_identity(nc, ident[:])
         mask = keep.tile([P, P], F32, name="mask")
@@ -101,9 +107,18 @@ def tile_columncorrelationhead_kernel(tc, column_embeddings, W, b, out):
             dst = wg[h][gd][:].rearrange("p (v f q t) -> p v f q t", v=2, f=2, q=P, t=4)[:, v, f]
             copy(engine, dst, src)
 
-        def w_quant(h, gd):
-            nc.vector.quantize_mx(out=wc[h][gd][:].bitcast(FP8X4), scales=ws[h][gd][:],
-                                  in_=wg[h][gd][:])
+        def w_quant(h, gd, v, halves):
+            words = slice(v * 256, (v + halves) * 256)
+            nc.vector.quantize_mx(out=wc[h][gd][:, words].bitcast(FP8X4), scales=ws[h][gd][:, words],
+                                  in_=wg[h][gd][:, v * 1024:(v + halves) * 1024])
+
+        def warm_up(passes):
+            scratch = mm_pool.tile([P, 512], F32, name="mm", tag="mm")
+            for k in range(passes):
+                nc.tensor.matmul_mx(out=scratch[:], lhsT=zero_codes[:, 0:P].bitcast(FP8X4),
+                                    lhsT_scale=zero_scales[:, 0:P],
+                                    rhs=zero_codes[:].bitcast(FP8X4), rhs_scale=zero_scales[:],
+                                    start=True, stop=True)
 
         def xw_place(n, ge):
             if (n, ge) in SOLO:
@@ -191,33 +206,38 @@ def tile_columncorrelationhead_kernel(tc, column_embeddings, W, b, out):
         load_x(13)
         load_x(14)
         load_x(15)
+        warm_up(5)
         transposes(0)
         t_copy(0, 0, "s")
         t_copy(0, 1, "v")
-        w_regroup(0, 0, 0, "s")
-        quant_x(0)
+        w_regroup(0, 0, 0, "v")
         w_regroup(0, 0, 1, "s")
         w_regroup(0, 0, 2, "v")
-        w_regroup(0, 0, 3, "v")
-        w_quant(0, 0)
-        w_regroup(0, 1, 0, "s")
-        w_regroup(0, 1, 1, "v")
-        w_regroup(0, 1, 2, "s")
-        w_regroup(0, 1, 3, "v")
-        w_quant(0, 1)
+        w_regroup(0, 0, 3, "s")
+        w_quant(0, 0, 0, 1)
+        w_quant(0, 0, 1, 1)
+        w_regroup(0, 1, 0, "v")
+        quant_x(0)
+        w_regroup(0, 1, 1, "s")
+        w_regroup(0, 1, 2, "v")
+        w_quant(0, 1, 0, 1)
+        w_regroup(0, 1, 3, "s")
+        w_quant(0, 1, 1, 1)
         nc.vector.tensor_copy(out=bias[:], in_=b_bf[:])
+        warm_up(5)
         transposes(1)
         t_copy(1, 0, "s")
         t_copy(1, 1, "v")
-        quant_x(1)
+        warm_up(2)
         first_matmul(0, 0, 0, "s")
-        first_matmul(0, 0, 1, "v")
+        first_matmul(0, 0, 1, "s")
         transposes(2)
         transposes(3)
+        quant_x(1)
         t_copy(2, 0, "s")
         t_copy(2, 1, "v")
         t_copy(3, 0, "s")
-        t_copy(3, 1, "v")
+        t_copy(3, 1, "s")
         quant_x(2)
         first_matmul(1, 0, 0, "s")
         quant_x(3)
@@ -229,34 +249,34 @@ def tile_columncorrelationhead_kernel(tc, column_embeddings, W, b, out):
         t_copy(4, 0, "v")
         t_copy(4, 1, "s")
         t_copy(5, 0, "v")
-        t_copy(5, 1, "s")
         quant_x(4)
+        w_regroup(1, 0, 3, "v")
+        t_copy(5, 1, "s")
         first_matmul(3, 0, 0, "s")
-        quant_x(5)
+        w_regroup(1, 0, 0, "s")
         first_matmul(3, 0, 1, "s")
-        w_regroup(1, 0, 0, "v")
         w_regroup(1, 0, 1, "v")
+        quant_x(5)
         first_matmul(4, 0, 0, "s")
         w_regroup(1, 0, 2, "v")
-        w_regroup(1, 0, 3, "v")
         first_matmul(4, 0, 1, "s")
-        w_quant(1, 0)
+        w_quant(1, 0, 0, 2)
         w_regroup(1, 1, 0, "v")
         first_matmul(5, 0, 0, "s")
-        w_regroup(1, 1, 1, "v")
-        w_regroup(1, 1, 2, "v")
         first_matmul(5, 0, 1, "s")
-        w_regroup(1, 1, 3, "v")
-        w_quant(1, 1)
         transposes(6)
+        w_regroup(1, 1, 2, "v")
+        w_regroup(1, 1, 1, "v")
         transposes(7)
         t_copy(6, 0, "s")
-        t_copy(6, 1, "s")
+        w_regroup(1, 1, 3, "v")
         t_copy(7, 0, "s")
+        w_quant(1, 1, 0, 2)
         t_copy(7, 1, "s")
-        quant_xw(0, 0, 2)
-        first_matmul(0, 1, 0, "v")
+        t_copy(6, 1, "v")
         quant_xw(2, 0, 2)
+        first_matmul(0, 1, 0, "v")
+        quant_xw(0, 0, 2)
         first_matmul(0, 1, 1, "s")
         quant_xw(4, 0, 2)
         first_matmul(1, 1, 0, "s")
@@ -264,27 +284,27 @@ def tile_columncorrelationhead_kernel(tc, column_embeddings, W, b, out):
         first_matmul(1, 1, 1, "s")
         quant_x(7)
         first_matmul(2, 1, 0, "s")
-        quant_xw(0, 1, 2)
-        first_matmul(2, 1, 1, "v")
+        first_matmul(2, 1, 1, "s")
         first_matmul(3, 1, 0, "s")
         first_matmul(3, 1, 1, "s")
+        quant_xw(0, 1, 2)
         second_matmul(0)
         quant_xw(2, 1, 2)
         second_matmul(1)
         first_matmul(4, 1, 0, "s")
-        finish(0)
         first_matmul(4, 1, 1, "s")
         finish(1)
         first_matmul(5, 1, 0, "v")
         first_matmul(5, 1, 1, "s")
-        quant_xw(4, 1, 2)
         second_matmul(2)
+        quant_xw(4, 1, 2)
+        finish(0)
         second_matmul(3)
         first_matmul(6, 0, 0, "s")
         first_matmul(6, 0, 1, "s")
         finish(2)
-        finish(3)
         first_matmul(7, 0, 0, "v")
+        finish(3)
         first_matmul(7, 0, 1, "s")
         second_matmul(4)
         quant_xw(6, 0, 2)
@@ -295,18 +315,18 @@ def tile_columncorrelationhead_kernel(tc, column_embeddings, W, b, out):
         t_copy(8, 1, "v")
         t_copy(9, 0, "s")
         t_copy(9, 1, "v")
-        first_matmul(6, 1, 0, "s")
         quant_x(8)
+        first_matmul(6, 1, 0, "s")
         first_matmul(6, 1, 1, "s")
-        first_matmul(7, 1, 0, "v")
-        quant_x(9)
         first_matmul(7, 1, 1, "s")
+        quant_x(9)
+        first_matmul(7, 1, 0, "v")
         quant_xw(6, 1, 2)
         first_matmul(8, 0, 0, "s")
         first_matmul(8, 0, 1, "s")
         finish(4)
-        finish(5)
         first_matmul(9, 0, 0, "v")
+        finish(5)
         first_matmul(9, 0, 1, "s")
         second_matmul(6)
         quant_xw(8, 0, 2)
@@ -317,18 +337,18 @@ def tile_columncorrelationhead_kernel(tc, column_embeddings, W, b, out):
         t_copy(10, 1, "v")
         t_copy(11, 0, "s")
         t_copy(11, 1, "v")
-        first_matmul(8, 1, 0, "s")
         quant_x(10)
+        first_matmul(8, 1, 0, "s")
         first_matmul(8, 1, 1, "s")
-        first_matmul(9, 1, 0, "v")
-        quant_x(11)
         first_matmul(9, 1, 1, "s")
+        quant_x(11)
+        first_matmul(9, 1, 0, "v")
         quant_xw(8, 1, 2)
         first_matmul(10, 0, 0, "s")
         first_matmul(10, 0, 1, "s")
         finish(6)
-        finish(7)
         first_matmul(11, 0, 0, "v")
+        finish(7)
         first_matmul(11, 0, 1, "s")
         second_matmul(8)
         quant_xw(10, 0, 2)
@@ -339,18 +359,18 @@ def tile_columncorrelationhead_kernel(tc, column_embeddings, W, b, out):
         t_copy(12, 1, "v")
         t_copy(13, 0, "s")
         t_copy(13, 1, "v")
-        first_matmul(10, 1, 0, "s")
         quant_x(12)
+        first_matmul(10, 1, 0, "s")
         first_matmul(10, 1, 1, "s")
-        first_matmul(11, 1, 0, "v")
-        quant_x(13)
         first_matmul(11, 1, 1, "s")
+        quant_x(13)
+        first_matmul(11, 1, 0, "v")
         quant_xw(10, 1, 2)
         first_matmul(12, 0, 0, "s")
         first_matmul(12, 0, 1, "s")
         finish(8)
-        finish(9)
         first_matmul(13, 0, 0, "v")
+        finish(9)
         first_matmul(13, 0, 1, "s")
         second_matmul(10)
         quant_xw(12, 0, 2)
@@ -361,12 +381,12 @@ def tile_columncorrelationhead_kernel(tc, column_embeddings, W, b, out):
         t_copy(14, 1, "v")
         t_copy(15, 0, "s")
         t_copy(15, 1, "v")
-        first_matmul(12, 1, 0, "s")
         quant_x(14)
+        first_matmul(12, 1, 0, "s")
         first_matmul(12, 1, 1, "s")
-        first_matmul(13, 1, 0, "v")
-        quant_x(15)
         first_matmul(13, 1, 1, "s")
+        quant_x(15)
+        first_matmul(13, 1, 0, "v")
         quant_xw(12, 1, 2)
         first_matmul(14, 0, 0, "s")
         first_matmul(14, 0, 1, "s")

@@ -32,8 +32,7 @@ def tile_columncorrelationhead_kernel(tc, column_embeddings, W, b, out):
         xwc_pool = ctx.enter_context(tc.tile_pool(name="xwc_pool", bufs=6))
         solo_pool = ctx.enter_context(tc.tile_pool(name="solo_pool", bufs=2))
         o_pool = ctx.enter_context(tc.tile_pool(name="o_pool", bufs=6))
-        tp_pool = ctx.enter_context(tc.psum_pool(name="tp_pool", bufs=4))
-        mm_pool = ctx.enter_context(tc.psum_pool(name="mm_pool", bufs=4))
+        psum = ctx.enter_context(tc.psum_pool(name="psum", bufs=8))
 
         def copy(engine, dst, src):
             if engine == "v":
@@ -81,7 +80,7 @@ def tile_columncorrelationhead_kernel(tc, column_embeddings, W, b, out):
         def transposes(n):
             x32 = xraw[n][:].bitcast(F32)
             for g in range(2):
-                tp = tp_pool.tile([P, 2, N], F32, name="tp", tag="tp")
+                tp = psum.tile([P, 2, N], F32, name="bank", tag="bank")
                 for u in range(2):
                     for rb in range(2):
                         lo = 256 * g + 128 * u
@@ -113,7 +112,7 @@ def tile_columncorrelationhead_kernel(tc, column_embeddings, W, b, out):
                                   in_=wg[h][gd][:, v * 1024:(v + halves) * 1024])
 
         def warm_up(passes):
-            scratch = mm_pool.tile([P, 512], F32, name="mm", tag="mm")
+            scratch = psum.tile([P, 512], F32, name="bank", tag="bank")
             for k in range(passes):
                 nc.tensor.matmul_mx(out=scratch[:], lhsT=zero_codes[:, 0:P].bitcast(FP8X4),
                                     lhsT_scale=zero_scales[:, 0:P],
@@ -125,18 +124,10 @@ def tile_columncorrelationhead_kernel(tc, column_embeddings, W, b, out):
                 return (n, ge), 0, 1
             return (n - n % 2, ge), n % 2, 2
 
-        def first_matmul(n, ge, ib, engine):
-            key, half, width = xw_place(n, ge)
-            if ("xwg", key) not in state:
-                if width == 1:
-                    state[("xwg", key)] = solo_pool.tile([P, N, 4], BF16, name="xwg1", tag="xwg1",
-                                                         align_bytes=64)
-                else:
-                    state[("xwg", key)] = xwg_pool.tile([P, 2 * N, 4], BF16, name="xwg", tag="xwg",
-                                                        align_bytes=64)
-            mm = mm_pool.tile([P, 512], F32, name="mm", tag="mm")
+        def first_matmul_passes(n, ge, ib, v):
+            mm = state[("mm", n, ge, ib)]
             cols = slice(ib * P, (ib + 1) * P)
-            for t in range(4):
+            for t in (2 * v, 2 * v + 1):
                 blk = slice(t * P, (t + 1) * P)
                 for gd in range(2):
                     nc.tensor.matmul_mx(out=mm[:, blk],
@@ -145,9 +136,24 @@ def tile_columncorrelationhead_kernel(tc, column_embeddings, W, b, out):
                                         rhs=xc[n][:, gd, cols].bitcast(FP8X4),
                                         rhs_scale=xs[n][:, gd, cols],
                                         start=(gd == 0), stop=(gd == 1))
+
+        def first_matmul_open(n, ge, ib):
+            state[("mm", n, ge, ib)] = psum.tile([P, 512], F32, name="bank", tag="bank")
+            first_matmul_passes(n, ge, ib, 0)
+
+        def first_matmul_close(n, ge, ib, engine):
+            first_matmul_passes(n, ge, ib, 1)
+            key, half, width = xw_place(n, ge)
+            if ("xwg", key) not in state:
+                if width == 1:
+                    state[("xwg", key)] = solo_pool.tile([P, N, 4], BF16, name="xwg1", tag="xwg1",
+                                                         align_bytes=64)
+                else:
+                    state[("xwg", key)] = xwg_pool.tile([P, 2 * N, 4], BF16, name="xwg", tag="xwg",
+                                                        align_bytes=64)
             lo = (2 * half + ib) * P
             copy(engine, state[("xwg", key)][:, lo:lo + P, :],
-                 mm[:].rearrange("p (t i) -> p i t", t=4))
+                 state[("mm", n, ge, ib)][:].rearrange("p (t i) -> p i t", t=4))
 
         def quant_xw(n, ge, width):
             key = xw_place(n, ge)[0]
@@ -164,7 +170,7 @@ def tile_columncorrelationhead_kernel(tc, column_embeddings, W, b, out):
         def second_matmul(n):
             o = o_pool.tile([P, 2, N], F32, name="o", tag="o")
             state[("o", n)] = o
-            mm = mm_pool.tile([P, 512], F32, name="mm", tag="mm")
+            mm = psum.tile([P, 512], F32, name="bank", tag="bank")
             for ib in range(2):
                 for ge in range(2):
                     key, half, width = xw_place(n, ge)
@@ -206,64 +212,75 @@ def tile_columncorrelationhead_kernel(tc, column_embeddings, W, b, out):
         load_x(13)
         load_x(14)
         load_x(15)
-        warm_up(5)
+        warm_up(6)
         transposes(0)
-        t_copy(0, 0, "s")
-        t_copy(0, 1, "v")
         w_regroup(0, 0, 0, "v")
-        w_regroup(0, 0, 1, "s")
+        w_regroup(0, 0, 1, "v")
         w_regroup(0, 0, 2, "v")
         w_regroup(0, 0, 3, "s")
+        t_copy(0, 0, "s")
+        t_copy(0, 1, "s")
+        warm_up(5)
         w_quant(0, 0, 0, 1)
         w_quant(0, 0, 1, 1)
-        w_regroup(0, 1, 0, "v")
+        w_regroup(0, 1, 0, "s")
+        w_regroup(0, 1, 1, "v")
         quant_x(0)
-        w_regroup(0, 1, 1, "s")
-        w_regroup(0, 1, 2, "v")
+        transposes(1)
         w_quant(0, 1, 0, 1)
+        w_regroup(0, 1, 2, "v")
         w_regroup(0, 1, 3, "s")
+        t_copy(1, 0, "s")
+        first_matmul_open(0, 0, 0)
+        first_matmul_open(0, 0, 1)
         w_quant(0, 1, 1, 1)
         nc.vector.tensor_copy(out=bias[:], in_=b_bf[:])
-        warm_up(5)
-        transposes(1)
-        t_copy(1, 0, "s")
         t_copy(1, 1, "v")
-        warm_up(2)
-        first_matmul(0, 0, 0, "s")
-        first_matmul(0, 0, 1, "s")
-        transposes(2)
-        transposes(3)
         quant_x(1)
+        first_matmul_close(0, 0, 0, "s")
+        first_matmul_close(0, 0, 1, "v")
+        transposes(2)
         t_copy(2, 0, "s")
         t_copy(2, 1, "v")
-        t_copy(3, 0, "s")
-        t_copy(3, 1, "s")
         quant_x(2)
-        first_matmul(1, 0, 0, "s")
-        quant_x(3)
-        first_matmul(1, 0, 1, "s")
-        first_matmul(2, 0, 0, "v")
-        first_matmul(2, 0, 1, "s")
+        first_matmul_open(1, 0, 0)
+        first_matmul_close(1, 0, 0, "v")
+        first_matmul_open(1, 0, 1)
+        first_matmul_close(1, 0, 1, "v")
+        transposes(3)
+        first_matmul_open(2, 0, 0)
+        first_matmul_close(2, 0, 0, "s")
+        first_matmul_open(2, 0, 1)
+        first_matmul_close(2, 0, 1, "s")
+        t_copy(3, 0, "v")
+        t_copy(3, 1, "v")
         transposes(4)
         transposes(5)
-        t_copy(4, 0, "v")
         t_copy(4, 1, "s")
-        t_copy(5, 0, "v")
-        quant_x(4)
-        w_regroup(1, 0, 3, "v")
+        t_copy(5, 0, "s")
+        quant_x(3)
         t_copy(5, 1, "s")
-        first_matmul(3, 0, 0, "s")
+        first_matmul_open(3, 0, 0)
+        first_matmul_close(3, 0, 0, "s")
+        w_regroup(1, 0, 3, "v")
         w_regroup(1, 0, 0, "s")
-        first_matmul(3, 0, 1, "s")
+        t_copy(4, 0, "v")
+        quant_x(4)
+        first_matmul_open(3, 0, 1)
+        first_matmul_close(3, 0, 1, "s")
         w_regroup(1, 0, 1, "v")
         quant_x(5)
-        first_matmul(4, 0, 0, "s")
+        first_matmul_open(4, 0, 0)
+        first_matmul_close(4, 0, 0, "s")
         w_regroup(1, 0, 2, "v")
-        first_matmul(4, 0, 1, "s")
+        first_matmul_open(4, 0, 1)
+        first_matmul_close(4, 0, 1, "s")
         w_quant(1, 0, 0, 2)
         w_regroup(1, 1, 0, "v")
-        first_matmul(5, 0, 0, "s")
-        first_matmul(5, 0, 1, "s")
+        first_matmul_open(5, 0, 0)
+        first_matmul_close(5, 0, 0, "s")
+        first_matmul_open(5, 0, 1)
+        first_matmul_close(5, 0, 1, "s")
         transposes(6)
         w_regroup(1, 1, 2, "v")
         w_regroup(1, 1, 1, "v")
@@ -275,37 +292,53 @@ def tile_columncorrelationhead_kernel(tc, column_embeddings, W, b, out):
         t_copy(7, 1, "s")
         t_copy(6, 1, "v")
         quant_xw(2, 0, 2)
-        first_matmul(0, 1, 0, "v")
+        first_matmul_open(0, 1, 0)
+        first_matmul_close(0, 1, 0, "v")
         quant_xw(0, 0, 2)
-        first_matmul(0, 1, 1, "s")
+        first_matmul_open(0, 1, 1)
+        first_matmul_close(0, 1, 1, "s")
         quant_xw(4, 0, 2)
-        first_matmul(1, 1, 0, "s")
+        first_matmul_open(1, 1, 0)
+        first_matmul_close(1, 1, 0, "s")
         quant_x(6)
-        first_matmul(1, 1, 1, "s")
+        first_matmul_open(1, 1, 1)
+        first_matmul_close(1, 1, 1, "s")
         quant_x(7)
-        first_matmul(2, 1, 0, "s")
-        first_matmul(2, 1, 1, "s")
-        first_matmul(3, 1, 0, "s")
-        first_matmul(3, 1, 1, "s")
+        first_matmul_open(2, 1, 0)
+        first_matmul_close(2, 1, 0, "s")
+        first_matmul_open(2, 1, 1)
+        first_matmul_close(2, 1, 1, "s")
+        first_matmul_open(3, 1, 0)
+        first_matmul_close(3, 1, 0, "s")
+        first_matmul_open(3, 1, 1)
+        first_matmul_close(3, 1, 1, "s")
         quant_xw(0, 1, 2)
         second_matmul(0)
         quant_xw(2, 1, 2)
         second_matmul(1)
-        first_matmul(4, 1, 0, "s")
-        first_matmul(4, 1, 1, "s")
+        first_matmul_open(4, 1, 0)
+        first_matmul_close(4, 1, 0, "s")
+        first_matmul_open(4, 1, 1)
+        first_matmul_close(4, 1, 1, "s")
         finish(1)
-        first_matmul(5, 1, 0, "v")
-        first_matmul(5, 1, 1, "s")
+        first_matmul_open(5, 1, 0)
+        first_matmul_close(5, 1, 0, "v")
+        first_matmul_open(5, 1, 1)
+        first_matmul_close(5, 1, 1, "s")
         second_matmul(2)
         quant_xw(4, 1, 2)
         finish(0)
         second_matmul(3)
-        first_matmul(6, 0, 0, "s")
-        first_matmul(6, 0, 1, "s")
+        first_matmul_open(6, 0, 0)
+        first_matmul_close(6, 0, 0, "s")
+        first_matmul_open(6, 0, 1)
+        first_matmul_close(6, 0, 1, "s")
         finish(2)
-        first_matmul(7, 0, 0, "v")
+        first_matmul_open(7, 0, 0)
+        first_matmul_close(7, 0, 0, "v")
         finish(3)
-        first_matmul(7, 0, 1, "s")
+        first_matmul_open(7, 0, 1)
+        first_matmul_close(7, 0, 1, "s")
         second_matmul(4)
         quant_xw(6, 0, 2)
         second_matmul(5)
@@ -316,18 +349,26 @@ def tile_columncorrelationhead_kernel(tc, column_embeddings, W, b, out):
         t_copy(9, 0, "s")
         t_copy(9, 1, "v")
         quant_x(8)
-        first_matmul(6, 1, 0, "s")
-        first_matmul(6, 1, 1, "s")
-        first_matmul(7, 1, 1, "s")
+        first_matmul_open(6, 1, 0)
+        first_matmul_close(6, 1, 0, "s")
+        first_matmul_open(6, 1, 1)
+        first_matmul_close(6, 1, 1, "s")
+        first_matmul_open(7, 1, 1)
+        first_matmul_close(7, 1, 1, "s")
         quant_x(9)
-        first_matmul(7, 1, 0, "v")
+        first_matmul_open(7, 1, 0)
+        first_matmul_close(7, 1, 0, "v")
         quant_xw(6, 1, 2)
-        first_matmul(8, 0, 0, "s")
-        first_matmul(8, 0, 1, "s")
+        first_matmul_open(8, 0, 0)
+        first_matmul_close(8, 0, 0, "s")
+        first_matmul_open(8, 0, 1)
+        first_matmul_close(8, 0, 1, "s")
         finish(4)
-        first_matmul(9, 0, 0, "v")
+        first_matmul_open(9, 0, 0)
+        first_matmul_close(9, 0, 0, "v")
         finish(5)
-        first_matmul(9, 0, 1, "s")
+        first_matmul_open(9, 0, 1)
+        first_matmul_close(9, 0, 1, "s")
         second_matmul(6)
         quant_xw(8, 0, 2)
         second_matmul(7)
@@ -338,18 +379,26 @@ def tile_columncorrelationhead_kernel(tc, column_embeddings, W, b, out):
         t_copy(11, 0, "s")
         t_copy(11, 1, "v")
         quant_x(10)
-        first_matmul(8, 1, 0, "s")
-        first_matmul(8, 1, 1, "s")
-        first_matmul(9, 1, 1, "s")
+        first_matmul_open(8, 1, 0)
+        first_matmul_close(8, 1, 0, "s")
+        first_matmul_open(8, 1, 1)
+        first_matmul_close(8, 1, 1, "s")
+        first_matmul_open(9, 1, 1)
+        first_matmul_close(9, 1, 1, "s")
         quant_x(11)
-        first_matmul(9, 1, 0, "v")
+        first_matmul_open(9, 1, 0)
+        first_matmul_close(9, 1, 0, "v")
         quant_xw(8, 1, 2)
-        first_matmul(10, 0, 0, "s")
-        first_matmul(10, 0, 1, "s")
+        first_matmul_open(10, 0, 0)
+        first_matmul_close(10, 0, 0, "s")
+        first_matmul_open(10, 0, 1)
+        first_matmul_close(10, 0, 1, "s")
         finish(6)
-        first_matmul(11, 0, 0, "v")
+        first_matmul_open(11, 0, 0)
+        first_matmul_close(11, 0, 0, "v")
         finish(7)
-        first_matmul(11, 0, 1, "s")
+        first_matmul_open(11, 0, 1)
+        first_matmul_close(11, 0, 1, "s")
         second_matmul(8)
         quant_xw(10, 0, 2)
         second_matmul(9)
@@ -360,18 +409,26 @@ def tile_columncorrelationhead_kernel(tc, column_embeddings, W, b, out):
         t_copy(13, 0, "s")
         t_copy(13, 1, "v")
         quant_x(12)
-        first_matmul(10, 1, 0, "s")
-        first_matmul(10, 1, 1, "s")
-        first_matmul(11, 1, 1, "s")
+        first_matmul_open(10, 1, 0)
+        first_matmul_close(10, 1, 0, "s")
+        first_matmul_open(10, 1, 1)
+        first_matmul_close(10, 1, 1, "s")
+        first_matmul_open(11, 1, 1)
+        first_matmul_close(11, 1, 1, "s")
         quant_x(13)
-        first_matmul(11, 1, 0, "v")
+        first_matmul_open(11, 1, 0)
+        first_matmul_close(11, 1, 0, "v")
         quant_xw(10, 1, 2)
-        first_matmul(12, 0, 0, "s")
-        first_matmul(12, 0, 1, "s")
+        first_matmul_open(12, 0, 0)
+        first_matmul_close(12, 0, 0, "s")
+        first_matmul_open(12, 0, 1)
+        first_matmul_close(12, 0, 1, "s")
         finish(8)
-        first_matmul(13, 0, 0, "v")
+        first_matmul_open(13, 0, 0)
+        first_matmul_close(13, 0, 0, "v")
         finish(9)
-        first_matmul(13, 0, 1, "s")
+        first_matmul_open(13, 0, 1)
+        first_matmul_close(13, 0, 1, "s")
         second_matmul(10)
         quant_xw(12, 0, 2)
         second_matmul(11)
@@ -382,24 +439,36 @@ def tile_columncorrelationhead_kernel(tc, column_embeddings, W, b, out):
         t_copy(15, 0, "s")
         t_copy(15, 1, "v")
         quant_x(14)
-        first_matmul(12, 1, 0, "s")
-        first_matmul(12, 1, 1, "s")
-        first_matmul(13, 1, 1, "s")
+        first_matmul_open(12, 1, 0)
+        first_matmul_close(12, 1, 0, "s")
+        first_matmul_open(12, 1, 1)
+        first_matmul_close(12, 1, 1, "s")
+        first_matmul_open(13, 1, 1)
+        first_matmul_close(13, 1, 1, "s")
         quant_x(15)
-        first_matmul(13, 1, 0, "v")
+        first_matmul_open(13, 1, 0)
+        first_matmul_close(13, 1, 0, "v")
         quant_xw(12, 1, 2)
-        first_matmul(14, 0, 0, "s")
-        first_matmul(14, 0, 1, "s")
+        first_matmul_open(14, 0, 0)
+        first_matmul_close(14, 0, 0, "s")
+        first_matmul_open(14, 0, 1)
+        first_matmul_close(14, 0, 1, "s")
         finish(10)
         finish(11)
-        first_matmul(15, 0, 0, "v")
-        first_matmul(15, 0, 1, "s")
+        first_matmul_open(15, 0, 0)
+        first_matmul_close(15, 0, 0, "v")
+        first_matmul_open(15, 0, 1)
+        first_matmul_close(15, 0, 1, "s")
         quant_xw(14, 0, 2)
-        first_matmul(14, 1, 0, "s")
-        first_matmul(14, 1, 1, "v")
-        first_matmul(15, 1, 0, "s")
+        first_matmul_open(14, 1, 0)
+        first_matmul_close(14, 1, 0, "s")
+        first_matmul_open(14, 1, 1)
+        first_matmul_close(14, 1, 1, "v")
+        first_matmul_open(15, 1, 0)
+        first_matmul_close(15, 1, 0, "s")
         quant_xw(14, 1, 1)
-        first_matmul(15, 1, 1, "v")
+        first_matmul_open(15, 1, 1)
+        first_matmul_close(15, 1, 1, "v")
         second_matmul(12)
         quant_xw(15, 1, 1)
         second_matmul(13)

@@ -5,17 +5,24 @@ from concourse.masks import make_identity
 
 F32 = mybir.dt.float32
 BF16 = mybir.dt.bfloat16
+I32 = mybir.dt.int32
 U32 = mybir.dt.uint32
 U8 = mybir.dt.uint8
-I32 = mybir.dt.int32
 FP8X4 = mybir.dt.float8_e4m3fn_x4
 ACT = mybir.ActivationFunctionType
 ALU = mybir.AluOpType
 
 P = 128
-B, N, D = 16, 256, 1024
-FLOPS = 2 * B * N * D * D + 2 * B * N * N * D
-SOLO = ((14, 1), (15, 1))
+BATCHES, ROWS, FEATURES = 16, 256, 1024
+PASS = 512
+PASSES = FEATURES // PASS
+GROUPS = 4
+BLOCKS = ROWS // P
+FLOPS = 2 * BATCHES * ROWS * FEATURES * FEATURES + 2 * BATCHES * ROWS * ROWS * FEATURES
+
+VECTOR, SCALAR = "vector", "scalar"
+
+QUANTISED_ALONE = ((14, 1), (15, 1))
 
 
 def tile_columncorrelationhead_kernel(tc, column_embeddings, W, b, out):
@@ -28,453 +35,327 @@ def tile_columncorrelationhead_kernel(tc, column_embeddings, W, b, out):
         ctx.enter_context(tc.manual_schedule())
         keep = ctx.enter_context(tc.tile_pool(name="keep", bufs=1))
         xg_pool = ctx.enter_context(tc.tile_pool(name="xg_pool", bufs=4))
-        xwg_pool = ctx.enter_context(tc.tile_pool(name="xwg_pool", bufs=5))
+        xwg_pool = ctx.enter_context(tc.tile_pool(name="xwg_pool", bufs=4))
         xwc_pool = ctx.enter_context(tc.tile_pool(name="xwc_pool", bufs=6))
         solo_pool = ctx.enter_context(tc.tile_pool(name="solo_pool", bufs=2))
         o_pool = ctx.enter_context(tc.tile_pool(name="o_pool", bufs=6))
         psum = ctx.enter_context(tc.psum_pool(name="psum", bufs=8))
 
         def copy(engine, dst, src):
-            if engine == "v":
+            if engine == VECTOR:
                 nc.vector.tensor_copy(out=dst, in_=src)
             else:
                 nc.scalar.copy(out=dst, in_=src)
 
-        zero_codes = keep.tile([P, 512], U32, name="zero_codes", align_bytes=64)
-        zero_scales = keep.tile([P, 512], U8, name="zero_scales", align_bytes=64)
-        zeros = keep.tile([P, 2048], BF16, name="zeros", align_bytes=64)
+        zero_codes = keep.tile([P, PASS], U32, name="zero_codes", align_bytes=64)
+        zero_scales = keep.tile([P, PASS], U8, name="zero_scales", align_bytes=64)
+        zeros = keep.tile([P, 4 * PASS], BF16, name="zeros", align_bytes=64)
         nc.vector.memset(zeros[:].bitcast(I32), 0)
         nc.vector.quantize_mx(out=zero_codes[:].bitcast(FP8X4), scales=zero_scales[:], in_=zeros[:])
         ident = keep.tile([P, P], F32, name="ident")
         make_identity(nc, ident[:])
-        mask = keep.tile([P, P], F32, name="mask")
-        nc.vector.tensor_scalar(out=mask[:], in0=ident[:], scalar1=2.0, scalar2=-1.0,
+        diag_mask = keep.tile([P, P], F32, name="diag_mask")
+        nc.vector.tensor_scalar(out=diag_mask[:], in0=ident[:], scalar1=2.0, scalar2=-1.0,
                                 op0=ALU.mult, op1=ALU.add)
-        b_bf = keep.tile([P, 1], BF16, name="b_bf")
-        nc.scalar.dma_start(out=b_bf[:], in_=b.partition_broadcast(P))
-        warm = keep.tile([P, 1], F32, name="warm")
-        nc.scalar.activation(out=warm[:], in_=ident[:, 0:1], func=ACT.Tanh)
+        b_bf16 = keep.tile([P, 1], BF16, name="b_bf16")
+        nc.scalar.dma_start(out=b_bf16[:], in_=b.partition_broadcast(P))
+        table_load = keep.tile([P, 1], F32, name="table_load")
+        nc.scalar.activation(out=table_load[:], in_=ident[:, 0:1], func=ACT.Tanh)
         bias = keep.tile([P, 1], F32, name="bias")
 
-        xraw = [keep.tile([P, 2, D], BF16, name="xraw%d" % n) for n in range(B)]
-        xc = [keep.tile([P, 2, N], U32, name="xc%d" % n, align_bytes=64) for n in range(B)]
-        xs = [keep.tile([P, 2, N], U8, name="xs%d" % n, align_bytes=64) for n in range(B)]
-        wraw = [[keep.tile([P, 2, 2, 512], BF16, name="wraw%d%d" % (h, gd)) for gd in range(2)]
-                for h in range(2)]
-        wg = [[keep.tile([P, 2048], BF16, name="wg%d%d" % (h, gd), align_bytes=64) for gd in range(2)]
-              for h in range(2)]
-        wc = [[keep.tile([P, 512], U32, name="wc%d%d" % (h, gd), align_bytes=64) for gd in range(2)]
-              for h in range(2)]
-        ws = [[keep.tile([P, 512], U8, name="ws%d%d" % (h, gd), align_bytes=64) for gd in range(2)]
-              for h in range(2)]
-        state = {}
+        x_raw = [keep.tile([P, BLOCKS, FEATURES], BF16, name="x_raw%d" % n) for n in range(BATCHES)]
+        x_codes = [keep.tile([P, PASSES, ROWS], U32, name="x_codes%d" % n, align_bytes=64)
+                   for n in range(BATCHES)]
+        x_scales = [keep.tile([P, PASSES, ROWS], U8, name="x_scales%d" % n, align_bytes=64)
+                    for n in range(BATCHES)]
+        w_raw, w_words, w_codes, w_scales = {}, {}, {}, {}
+        for s in range(PASSES):
+            for g in range(PASSES):
+                w_raw[s, g] = keep.tile([P, 2, 2, PASS], BF16, name="w_raw%d%d" % (s, g))
+                w_words[s, g] = keep.tile([P, 4 * PASS], BF16, name="w_words%d%d" % (s, g),
+                                          align_bytes=64)
+                w_codes[s, g] = keep.tile([P, PASS], U32, name="w_codes%d%d" % (s, g),
+                                          align_bytes=64)
+                w_scales[s, g] = keep.tile([P, PASS], U8, name="w_scales%d%d" % (s, g),
+                                           align_bytes=64)
+        live = {}
 
         def load_x(n):
-            nc.sync.dma_start(out=xraw[n][:], in_=x_rows[:, 2 * n:2 * n + 2, :])
+            nc.sync.dma_start(out=x_raw[n][:], in_=x_rows[:, BLOCKS * n:BLOCKS * (n + 1), :])
 
-        def load_w(h, gd):
+        def load_w(s, g):
             for e in range(2):
-                nc.sync.dma_start(out=wraw[h][gd][:, :, e, :],
-                                  in_=w_view[:, 2 * gd:2 * gd + 2, e, h * 512:(h + 1) * 512])
-
-        def transposes(n):
-            x32 = xraw[n][:].bitcast(F32)
-            for g in range(2):
-                tp = psum.tile([P, 2, N], F32, name="bank", tag="bank")
-                for u in range(2):
-                    for rb in range(2):
-                        lo = 256 * g + 128 * u
-                        nc.tensor.transpose(tp[:, u, rb * P:(rb + 1) * P],
-                                            x32[:, rb, lo:lo + P], ident[:])
-                state[("tp", n, g)] = tp
-            state[("xg", n)] = xg_pool.tile([P, 2, 4 * N], BF16, name="xg", tag="xg", align_bytes=64)
-
-        def t_copy(n, g, engine):
-            xg32 = state[("xg", n)][:].bitcast(F32)
-            copy(engine, xg32[:, g, :].rearrange("p (i u) -> p i u", u=2),
-                 state[("tp", n, g)][:].rearrange("p u i -> p i u"))
-
-        def quant_x(n):
-            nc.vector.quantize_mx(out=xc[n][:].rearrange("p g i -> p (g i)").bitcast(FP8X4),
-                                  scales=xs[n][:].rearrange("p g i -> p (g i)"),
-                                  in_=state[("xg", n)][:].rearrange("p g c -> p (g c)"))
-
-        def w_regroup(h, gd, piece, engine):
-            v, f = divmod(piece, 2)
-            src = wraw[h][gd][:].rearrange("p u e c -> p (u e) c")
-            src = src.rearrange("p t (v q f) -> p v f q t", v=2, q=P, f=2)[:, v, f]
-            dst = wg[h][gd][:].rearrange("p (v f q t) -> p v f q t", v=2, f=2, q=P, t=4)[:, v, f]
-            copy(engine, dst, src)
-
-        def w_quant(h, gd, v, halves):
-            words = slice(v * 256, (v + halves) * 256)
-            nc.vector.quantize_mx(out=wc[h][gd][:, words].bitcast(FP8X4), scales=ws[h][gd][:, words],
-                                  in_=wg[h][gd][:, v * 1024:(v + halves) * 1024])
+                nc.sync.dma_start(out=w_raw[s, g][:, :, e, :],
+                                  in_=w_view[:, 2 * g:2 * g + 2, e, s * PASS:(s + 1) * PASS])
 
         def warm_up(passes):
-            scratch = psum.tile([P, 512], F32, name="bank", tag="bank")
+            scratch = psum.tile([P, PASS], F32, name="bank", tag="bank")
             for k in range(passes):
                 nc.tensor.matmul_mx(out=scratch[:], lhsT=zero_codes[:, 0:P].bitcast(FP8X4),
                                     lhsT_scale=zero_scales[:, 0:P],
                                     rhs=zero_codes[:].bitcast(FP8X4), rhs_scale=zero_scales[:],
                                     start=True, stop=True)
 
-        def xw_place(n, ge):
-            if (n, ge) in SOLO:
-                return (n, ge), 0, 1
-            return (n - n % 2, ge), n % 2, 2
+        def transposes(n):
+            pairs = x_raw[n][:].bitcast(F32)
+            for g in range(PASSES):
+                bank = psum.tile([P, 2, ROWS], F32, name="bank", tag="bank")
+                for u in range(2):
+                    for block in range(BLOCKS):
+                        lo = (PASS // 2) * g + P * u
+                        nc.tensor.transpose(bank[:, u, block * P:(block + 1) * P],
+                                            pairs[:, block, lo:lo + P], ident[:])
+                live["xT", n, g] = bank
+            live["xg", n] = xg_pool.tile([P, PASSES, 4 * ROWS], BF16, name="xg", tag="xg",
+                                         align_bytes=64)
 
-        def first_matmul_passes(n, ge, ib, v):
-            mm = state[("mm", n, ge, ib)]
-            cols = slice(ib * P, (ib + 1) * P)
-            for t in (2 * v, 2 * v + 1):
-                blk = slice(t * P, (t + 1) * P)
-                for gd in range(2):
-                    nc.tensor.matmul_mx(out=mm[:, blk],
-                                        lhsT=wc[ge][gd][:, blk].bitcast(FP8X4),
-                                        lhsT_scale=ws[ge][gd][:, blk],
-                                        rhs=xc[n][:, gd, cols].bitcast(FP8X4),
-                                        rhs_scale=xs[n][:, gd, cols],
-                                        start=(gd == 0), stop=(gd == 1))
+        def copy_transposed(n, g, engine):
+            pairs = live["xg", n][:].bitcast(F32)
+            copy(engine, pairs[:, g, :].rearrange("p (i u) -> p i u", u=2),
+                 live["xT", n, g][:].rearrange("p u i -> p i u"))
 
-        def first_matmul_open(n, ge, ib):
-            state[("mm", n, ge, ib)] = psum.tile([P, 512], F32, name="bank", tag="bank")
-            first_matmul_passes(n, ge, ib, 0)
+        def quantise_x(n):
+            nc.vector.quantize_mx(out=x_codes[n][:].rearrange("p g i -> p (g i)").bitcast(FP8X4),
+                                  scales=x_scales[n][:].rearrange("p g i -> p (g i)"),
+                                  in_=live["xg", n][:].rearrange("p g c -> p (g c)"))
 
-        def first_matmul_close(n, ge, ib, engine):
-            first_matmul_passes(n, ge, ib, 1)
-            key, half, width = xw_place(n, ge)
-            if ("xwg", key) not in state:
-                if width == 1:
-                    state[("xwg", key)] = solo_pool.tile([P, N, 4], BF16, name="xwg1", tag="xwg1",
-                                                         align_bytes=64)
+        def regroup_w(s, g, group, engine):
+            v, f = divmod(group, 2)
+            src = w_raw[s, g][:].rearrange("p u e c -> p (u e) c")
+            src = src.rearrange("p t (v q f) -> p v f q t", v=2, q=P, f=2)[:, v, f]
+            dst = w_words[s, g][:].rearrange("p (v f q t) -> p v f q t", v=2, f=2, q=P, t=4)[:, v, f]
+            copy(engine, dst, src)
+
+        def quantise_w(s, g, first_group, groups):
+            words = slice(first_group * P, (first_group + groups) * P)
+            nc.vector.quantize_mx(out=w_codes[s, g][:, words].bitcast(FP8X4),
+                                  scales=w_scales[s, g][:, words],
+                                  in_=w_words[s, g][:, 4 * first_group * P:4 * (first_group + groups) * P])
+
+        def first_matmul_groups(n, s, block, groups):
+            bank = live["xwT", n, s, block]
+            rows = slice(block * P, (block + 1) * P)
+            for t in groups:
+                cols = slice(t * P, (t + 1) * P)
+                for g in range(PASSES):
+                    nc.tensor.matmul_mx(out=bank[:, cols],
+                                        lhsT=w_codes[s, g][:, cols].bitcast(FP8X4),
+                                        lhsT_scale=w_scales[s, g][:, cols],
+                                        rhs=x_codes[n][:, g, rows].bitcast(FP8X4),
+                                        rhs_scale=x_scales[n][:, g, rows],
+                                        start=(g == 0), stop=(g == PASSES - 1))
+
+        def first_matmul_open(n, s, block):
+            live["xwT", n, s, block] = psum.tile([P, PASS], F32, name="bank", tag="bank")
+            first_matmul_groups(n, s, block, (0, 1))
+
+        def xw_place(n, s):
+            if (n, s) in QUANTISED_ALONE:
+                return (n, s), 0, 1
+            return (n - n % 2, s), n % 2, 2
+
+        def first_matmul_close(n, s, block, engine):
+            first_matmul_groups(n, s, block, (2, 3))
+            key, place, batches = xw_place(n, s)
+            if ("xwg", key) not in live:
+                if batches == 1:
+                    live["xwg", key] = solo_pool.tile([P, ROWS, 4], BF16, name="xwg1", tag="xwg1",
+                                                      align_bytes=64)
                 else:
-                    state[("xwg", key)] = xwg_pool.tile([P, 2 * N, 4], BF16, name="xwg", tag="xwg",
-                                                        align_bytes=64)
-            lo = (2 * half + ib) * P
-            copy(engine, state[("xwg", key)][:, lo:lo + P, :],
-                 state[("mm", n, ge, ib)][:].rearrange("p (t i) -> p i t", t=4))
+                    live["xwg", key] = xwg_pool.tile([P, 2 * ROWS, 4], BF16, name="xwg", tag="xwg",
+                                                     align_bytes=64)
+            lo = (BLOCKS * place + block) * P
+            copy(engine, live["xwg", key][:, lo:lo + P, :],
+                 live["xwT", n, s, block][:].rearrange("p (t i) -> p i t", t=GROUPS))
 
-        def quant_xw(n, ge, width):
-            key = xw_place(n, ge)[0]
-            if width == 1:
-                codes = solo_pool.tile([P, N], U32, name="xwc1", tag="xwc1", align_bytes=64)
-                planes = solo_pool.tile([P, N], U8, name="xws1", tag="xws1", align_bytes=64)
+        def first_matmul(n, s, block, engine):
+            first_matmul_open(n, s, block)
+            first_matmul_close(n, s, block, engine)
+
+        def quantise_xw(n, s):
+            key, place, batches = xw_place(n, s)
+            if batches == 1:
+                codes = solo_pool.tile([P, ROWS], U32, name="xwc1", tag="xwc1", align_bytes=64)
+                scales = solo_pool.tile([P, ROWS], U8, name="xws1", tag="xws1", align_bytes=64)
             else:
-                codes = xwc_pool.tile([P, 2 * N], U32, name="xwc", tag="xwc", align_bytes=64)
-                planes = xwc_pool.tile([P, 2 * N], U8, name="xws", tag="xws", align_bytes=64)
-            nc.vector.quantize_mx(out=codes[:].bitcast(FP8X4), scales=planes[:],
-                                  in_=state[("xwg", key)][:].rearrange("p i t -> p (i t)"))
-            state[("xwc", key)] = (codes, planes)
+                codes = xwc_pool.tile([P, 2 * ROWS], U32, name="xwc", tag="xwc", align_bytes=64)
+                scales = xwc_pool.tile([P, 2 * ROWS], U8, name="xws", tag="xws", align_bytes=64)
+            nc.vector.quantize_mx(out=codes[:].bitcast(FP8X4), scales=scales[:],
+                                  in_=live["xwg", key][:].rearrange("p i t -> p (i t)"))
+            live["xwc", key] = (codes, scales)
 
         def second_matmul(n):
-            o = o_pool.tile([P, 2, N], F32, name="o", tag="o")
-            state[("o", n)] = o
-            mm = psum.tile([P, 512], F32, name="bank", tag="bank")
-            for ib in range(2):
-                for ge in range(2):
-                    key, half, width = xw_place(n, ge)
-                    codes, planes = state[("xwc", key)]
-                    blk = slice((2 * half + ib) * P, (2 * half + ib + 1) * P)
-                    nc.tensor.matmul_mx(out=mm[:, ib * N:(ib + 1) * N],
-                                        lhsT=codes[:, blk].bitcast(FP8X4),
-                                        lhsT_scale=planes[:, blk],
-                                        rhs=xc[n][:, ge, :].bitcast(FP8X4),
-                                        rhs_scale=xs[n][:, ge, :],
-                                        start=(ge == 0), stop=(ge == 1))
-            nc.scalar.activation(out=o[:], in_=mm[:].rearrange("p (r j) -> p r j", r=2),
+            result = o_pool.tile([P, BLOCKS, ROWS], F32, name="o", tag="o")
+            live["o", n] = result
+            bank = psum.tile([P, PASS], F32, name="bank", tag="bank")
+            for block in range(BLOCKS):
+                for s in range(PASSES):
+                    key, place, batches = xw_place(n, s)
+                    codes, scales = live["xwc", key]
+                    rows = slice((BLOCKS * place + block) * P, (BLOCKS * place + block + 1) * P)
+                    nc.tensor.matmul_mx(out=bank[:, block * ROWS:(block + 1) * ROWS],
+                                        lhsT=codes[:, rows].bitcast(FP8X4),
+                                        lhsT_scale=scales[:, rows],
+                                        rhs=x_codes[n][:, s, :].bitcast(FP8X4),
+                                        rhs_scale=x_scales[n][:, s, :],
+                                        start=(s == 0), stop=(s == PASSES - 1))
+            nc.scalar.activation(out=result[:], in_=bank[:].rearrange("p (r j) -> p r j", r=BLOCKS),
                                  func=ACT.Tanh, bias=bias[:, 0:1], scale=1.0)
 
         def finish(n):
-            o = state[("o", n)]
-            diag = o[:].rearrange("p r (a k) -> p (r a) k", k=P)[:, 0:4:3, :]
-            nc.vector.tensor_tensor(out=diag, in0=diag,
-                                    in1=mask[:].unsqueeze(1).to_broadcast([P, 2, P]), op=ALU.max)
-            nc.sync.dma_start(out=out_rows[:, 2 * n:2 * n + 2, :], in_=o[:])
+            result = live["o", n]
+            diagonal = result[:].rearrange("p r (a k) -> p (r a) k", k=P)[:, 0:4:3, :]
+            nc.vector.tensor_tensor(out=diagonal, in0=diagonal,
+                                    in1=diag_mask[:].unsqueeze(1).to_broadcast([P, BLOCKS, P]),
+                                    op=ALU.max)
+            nc.sync.dma_start(out=out_rows[:, BLOCKS * n:BLOCKS * (n + 1), :], in_=result[:])
 
         load_x(0)
         load_w(0, 0)
         load_w(0, 1)
-        load_x(1)
-        load_x(2)
-        load_x(3)
-        load_x(4)
-        load_x(5)
+        for n in range(1, 6):
+            load_x(n)
         load_w(1, 0)
         load_w(1, 1)
-        load_x(6)
-        load_x(7)
-        load_x(8)
-        load_x(9)
-        load_x(10)
-        load_x(11)
-        load_x(12)
-        load_x(13)
-        load_x(14)
-        load_x(15)
+        for n in range(6, BATCHES):
+            load_x(n)
+
         warm_up(6)
         transposes(0)
-        w_regroup(0, 0, 0, "v")
-        w_regroup(0, 0, 1, "v")
-        w_regroup(0, 0, 2, "v")
-        w_regroup(0, 0, 3, "s")
-        t_copy(0, 0, "s")
-        t_copy(0, 1, "s")
+        for group, engine in ((0, VECTOR), (1, VECTOR), (2, VECTOR), (3, SCALAR)):
+            regroup_w(0, 0, group, engine)
+        copy_transposed(0, 0, SCALAR)
+        copy_transposed(0, 1, SCALAR)
         warm_up(5)
-        w_quant(0, 0, 0, 1)
-        w_quant(0, 0, 1, 1)
-        w_regroup(0, 1, 0, "s")
-        w_regroup(0, 1, 1, "v")
-        quant_x(0)
+        quantise_w(0, 0, 0, 2)
+        quantise_w(0, 0, 2, 2)
+        regroup_w(0, 1, 0, SCALAR)
+        regroup_w(0, 1, 1, VECTOR)
+        quantise_x(0)
         transposes(1)
-        w_quant(0, 1, 0, 1)
-        w_regroup(0, 1, 2, "v")
-        w_regroup(0, 1, 3, "s")
-        t_copy(1, 0, "s")
+        quantise_w(0, 1, 0, 2)
+        regroup_w(0, 1, 2, VECTOR)
+        regroup_w(0, 1, 3, SCALAR)
+        copy_transposed(1, 0, SCALAR)
         first_matmul_open(0, 0, 0)
         first_matmul_open(0, 0, 1)
-        w_quant(0, 1, 1, 1)
-        nc.vector.tensor_copy(out=bias[:], in_=b_bf[:])
-        t_copy(1, 1, "v")
-        quant_x(1)
-        first_matmul_close(0, 0, 0, "s")
-        first_matmul_close(0, 0, 1, "v")
+        quantise_w(0, 1, 2, 2)
+        nc.vector.tensor_copy(out=bias[:], in_=b_bf16[:])
+        copy_transposed(1, 1, VECTOR)
+        quantise_x(1)
+        first_matmul_close(0, 0, 0, SCALAR)
+        first_matmul_close(0, 0, 1, VECTOR)
+
         transposes(2)
-        t_copy(2, 0, "s")
-        t_copy(2, 1, "v")
-        quant_x(2)
-        first_matmul_open(1, 0, 0)
-        first_matmul_close(1, 0, 0, "v")
-        first_matmul_open(1, 0, 1)
-        first_matmul_close(1, 0, 1, "v")
+        copy_transposed(2, 0, SCALAR)
+        copy_transposed(2, 1, VECTOR)
+        quantise_x(2)
+        first_matmul(1, 0, 0, VECTOR)
+        first_matmul(1, 0, 1, VECTOR)
         transposes(3)
-        first_matmul_open(2, 0, 0)
-        first_matmul_close(2, 0, 0, "s")
-        first_matmul_open(2, 0, 1)
-        first_matmul_close(2, 0, 1, "s")
-        t_copy(3, 0, "v")
-        t_copy(3, 1, "v")
+        first_matmul(2, 0, 0, SCALAR)
+        first_matmul(2, 0, 1, SCALAR)
+        copy_transposed(3, 0, VECTOR)
+        copy_transposed(3, 1, VECTOR)
         transposes(4)
         transposes(5)
-        t_copy(4, 1, "s")
-        t_copy(5, 0, "s")
-        quant_x(3)
-        t_copy(5, 1, "s")
-        first_matmul_open(3, 0, 0)
-        first_matmul_close(3, 0, 0, "s")
-        w_regroup(1, 0, 3, "v")
-        w_regroup(1, 0, 0, "s")
-        t_copy(4, 0, "v")
-        quant_x(4)
-        first_matmul_open(3, 0, 1)
-        first_matmul_close(3, 0, 1, "s")
-        w_regroup(1, 0, 1, "v")
-        quant_x(5)
-        first_matmul_open(4, 0, 0)
-        first_matmul_close(4, 0, 0, "s")
-        w_regroup(1, 0, 2, "v")
-        first_matmul_open(4, 0, 1)
-        first_matmul_close(4, 0, 1, "s")
-        w_quant(1, 0, 0, 2)
-        w_regroup(1, 1, 0, "v")
-        first_matmul_open(5, 0, 0)
-        first_matmul_close(5, 0, 0, "s")
-        first_matmul_open(5, 0, 1)
-        first_matmul_close(5, 0, 1, "s")
+        copy_transposed(4, 1, SCALAR)
+        copy_transposed(5, 0, SCALAR)
+        quantise_x(3)
+        copy_transposed(5, 1, SCALAR)
+        first_matmul(3, 0, 0, SCALAR)
+        regroup_w(1, 0, 1, VECTOR)
+        regroup_w(1, 0, 0, SCALAR)
+        copy_transposed(4, 0, VECTOR)
+        quantise_x(4)
+        first_matmul(3, 0, 1, SCALAR)
+        regroup_w(1, 0, 2, VECTOR)
+        quantise_x(5)
+        first_matmul(4, 0, 0, SCALAR)
+        regroup_w(1, 0, 3, VECTOR)
+        first_matmul(4, 0, 1, SCALAR)
+        quantise_w(1, 0, 0, GROUPS)
+        regroup_w(1, 1, 0, VECTOR)
+        first_matmul(5, 0, 0, SCALAR)
+        first_matmul(5, 0, 1, SCALAR)
         transposes(6)
-        w_regroup(1, 1, 2, "v")
-        w_regroup(1, 1, 1, "v")
         transposes(7)
-        t_copy(6, 0, "s")
-        w_regroup(1, 1, 3, "v")
-        t_copy(7, 0, "s")
-        w_quant(1, 1, 0, 2)
-        t_copy(7, 1, "s")
-        t_copy(6, 1, "v")
-        quant_xw(2, 0, 2)
-        first_matmul_open(0, 1, 0)
-        first_matmul_close(0, 1, 0, "v")
-        quant_xw(0, 0, 2)
-        first_matmul_open(0, 1, 1)
-        first_matmul_close(0, 1, 1, "s")
-        quant_xw(4, 0, 2)
-        first_matmul_open(1, 1, 0)
-        first_matmul_close(1, 1, 0, "s")
-        quant_x(6)
-        first_matmul_open(1, 1, 1)
-        first_matmul_close(1, 1, 1, "s")
-        quant_x(7)
-        first_matmul_open(2, 1, 0)
-        first_matmul_close(2, 1, 0, "s")
-        first_matmul_open(2, 1, 1)
-        first_matmul_close(2, 1, 1, "s")
-        first_matmul_open(3, 1, 0)
-        first_matmul_close(3, 1, 0, "s")
-        first_matmul_open(3, 1, 1)
-        first_matmul_close(3, 1, 1, "s")
-        quant_xw(0, 1, 2)
+        regroup_w(1, 1, 1, VECTOR)
+        regroup_w(1, 1, 2, VECTOR)
+        copy_transposed(6, 0, SCALAR)
+        regroup_w(1, 1, 3, VECTOR)
+        copy_transposed(7, 0, SCALAR)
+        quantise_w(1, 1, 0, GROUPS)
+        copy_transposed(7, 1, SCALAR)
+        copy_transposed(6, 1, VECTOR)
+
+        quantise_xw(0, 0)
+        first_matmul(0, 1, 0, VECTOR)
+        quantise_xw(2, 0)
+        first_matmul(0, 1, 1, SCALAR)
+        quantise_xw(4, 0)
+        first_matmul(1, 1, 0, SCALAR)
+        quantise_x(6)
+        first_matmul(1, 1, 1, SCALAR)
+        quantise_x(7)
+        for n in (2, 3):
+            for block in range(BLOCKS):
+                first_matmul(n, 1, block, SCALAR)
+        quantise_xw(0, 1)
         second_matmul(0)
-        quant_xw(2, 1, 2)
+        quantise_xw(2, 1)
         second_matmul(1)
-        first_matmul_open(4, 1, 0)
-        first_matmul_close(4, 1, 0, "s")
-        first_matmul_open(4, 1, 1)
-        first_matmul_close(4, 1, 1, "s")
-        finish(1)
-        first_matmul_open(5, 1, 0)
-        first_matmul_close(5, 1, 0, "v")
-        first_matmul_open(5, 1, 1)
-        first_matmul_close(5, 1, 1, "s")
-        second_matmul(2)
-        quant_xw(4, 1, 2)
+        first_matmul(4, 1, 0, SCALAR)
+        first_matmul(4, 1, 1, SCALAR)
         finish(0)
+        first_matmul(5, 1, 0, VECTOR)
+        first_matmul(5, 1, 1, SCALAR)
+        second_matmul(2)
+        quantise_xw(4, 1)
+        finish(1)
         second_matmul(3)
-        first_matmul_open(6, 0, 0)
-        first_matmul_close(6, 0, 0, "s")
-        first_matmul_open(6, 0, 1)
-        first_matmul_close(6, 0, 1, "s")
-        finish(2)
-        first_matmul_open(7, 0, 0)
-        first_matmul_close(7, 0, 0, "v")
-        finish(3)
-        first_matmul_open(7, 0, 1)
-        first_matmul_close(7, 0, 1, "s")
-        second_matmul(4)
-        quant_xw(6, 0, 2)
-        second_matmul(5)
-        transposes(8)
-        transposes(9)
-        t_copy(8, 0, "v")
-        t_copy(8, 1, "v")
-        t_copy(9, 0, "s")
-        t_copy(9, 1, "v")
-        quant_x(8)
-        first_matmul_open(6, 1, 0)
-        first_matmul_close(6, 1, 0, "s")
-        first_matmul_open(6, 1, 1)
-        first_matmul_close(6, 1, 1, "s")
-        first_matmul_open(7, 1, 1)
-        first_matmul_close(7, 1, 1, "s")
-        quant_x(9)
-        first_matmul_open(7, 1, 0)
-        first_matmul_close(7, 1, 0, "v")
-        quant_xw(6, 1, 2)
-        first_matmul_open(8, 0, 0)
-        first_matmul_close(8, 0, 0, "s")
-        first_matmul_open(8, 0, 1)
-        first_matmul_close(8, 0, 1, "s")
-        finish(4)
-        first_matmul_open(9, 0, 0)
-        first_matmul_close(9, 0, 0, "v")
-        finish(5)
-        first_matmul_open(9, 0, 1)
-        first_matmul_close(9, 0, 1, "s")
-        second_matmul(6)
-        quant_xw(8, 0, 2)
-        second_matmul(7)
-        transposes(10)
-        transposes(11)
-        t_copy(10, 0, "v")
-        t_copy(10, 1, "v")
-        t_copy(11, 0, "s")
-        t_copy(11, 1, "v")
-        quant_x(10)
-        first_matmul_open(8, 1, 0)
-        first_matmul_close(8, 1, 0, "s")
-        first_matmul_open(8, 1, 1)
-        first_matmul_close(8, 1, 1, "s")
-        first_matmul_open(9, 1, 1)
-        first_matmul_close(9, 1, 1, "s")
-        quant_x(11)
-        first_matmul_open(9, 1, 0)
-        first_matmul_close(9, 1, 0, "v")
-        quant_xw(8, 1, 2)
-        first_matmul_open(10, 0, 0)
-        first_matmul_close(10, 0, 0, "s")
-        first_matmul_open(10, 0, 1)
-        first_matmul_close(10, 0, 1, "s")
-        finish(6)
-        first_matmul_open(11, 0, 0)
-        first_matmul_close(11, 0, 0, "v")
-        finish(7)
-        first_matmul_open(11, 0, 1)
-        first_matmul_close(11, 0, 1, "s")
-        second_matmul(8)
-        quant_xw(10, 0, 2)
-        second_matmul(9)
-        transposes(12)
-        transposes(13)
-        t_copy(12, 0, "v")
-        t_copy(12, 1, "v")
-        t_copy(13, 0, "s")
-        t_copy(13, 1, "v")
-        quant_x(12)
-        first_matmul_open(10, 1, 0)
-        first_matmul_close(10, 1, 0, "s")
-        first_matmul_open(10, 1, 1)
-        first_matmul_close(10, 1, 1, "s")
-        first_matmul_open(11, 1, 1)
-        first_matmul_close(11, 1, 1, "s")
-        quant_x(13)
-        first_matmul_open(11, 1, 0)
-        first_matmul_close(11, 1, 0, "v")
-        quant_xw(10, 1, 2)
-        first_matmul_open(12, 0, 0)
-        first_matmul_close(12, 0, 0, "s")
-        first_matmul_open(12, 0, 1)
-        first_matmul_close(12, 0, 1, "s")
-        finish(8)
-        first_matmul_open(13, 0, 0)
-        first_matmul_close(13, 0, 0, "v")
-        finish(9)
-        first_matmul_open(13, 0, 1)
-        first_matmul_close(13, 0, 1, "s")
-        second_matmul(10)
-        quant_xw(12, 0, 2)
-        second_matmul(11)
-        transposes(14)
-        transposes(15)
-        t_copy(14, 0, "v")
-        t_copy(14, 1, "v")
-        t_copy(15, 0, "s")
-        t_copy(15, 1, "v")
-        quant_x(14)
-        first_matmul_open(12, 1, 0)
-        first_matmul_close(12, 1, 0, "s")
-        first_matmul_open(12, 1, 1)
-        first_matmul_close(12, 1, 1, "s")
-        first_matmul_open(13, 1, 1)
-        first_matmul_close(13, 1, 1, "s")
-        quant_x(15)
-        first_matmul_open(13, 1, 0)
-        first_matmul_close(13, 1, 0, "v")
-        quant_xw(12, 1, 2)
-        first_matmul_open(14, 0, 0)
-        first_matmul_close(14, 0, 0, "s")
-        first_matmul_open(14, 0, 1)
-        first_matmul_close(14, 0, 1, "s")
-        finish(10)
-        finish(11)
-        first_matmul_open(15, 0, 0)
-        first_matmul_close(15, 0, 0, "v")
-        first_matmul_open(15, 0, 1)
-        first_matmul_close(15, 0, 1, "s")
-        quant_xw(14, 0, 2)
-        first_matmul_open(14, 1, 0)
-        first_matmul_close(14, 1, 0, "s")
-        first_matmul_open(14, 1, 1)
-        first_matmul_close(14, 1, 1, "v")
-        first_matmul_open(15, 1, 0)
-        first_matmul_close(15, 1, 0, "s")
-        quant_xw(14, 1, 1)
-        first_matmul_open(15, 1, 1)
-        first_matmul_close(15, 1, 1, "v")
-        second_matmul(12)
-        quant_xw(15, 1, 1)
-        second_matmul(13)
-        second_matmul(14)
-        finish(12)
-        second_matmul(15)
-        finish(13)
-        finish(14)
-        finish(15)
+
+        def pass_0(a):
+            first_matmul(a, 0, 0, SCALAR)
+            first_matmul(a, 0, 1, SCALAR)
+            finish(a - 4)
+            first_matmul(a + 1, 0, 0, VECTOR)
+            finish(a - 3)
+            first_matmul(a + 1, 0, 1, SCALAR)
+
+        last = BATCHES - 2
+        for a in range(6, last, 2):
+            pass_0(a)
+            second_matmul(a - 2)
+            quantise_xw(a, 0)
+            second_matmul(a - 1)
+            transposes(a + 2)
+            transposes(a + 3)
+            copy_transposed(a + 2, 0, VECTOR)
+            copy_transposed(a + 2, 1, VECTOR)
+            copy_transposed(a + 3, 0, SCALAR)
+            copy_transposed(a + 3, 1, VECTOR)
+            quantise_x(a + 2)
+            first_matmul(a, 1, 0, SCALAR)
+            first_matmul(a, 1, 1, SCALAR)
+            quantise_x(a + 3)
+            first_matmul(a + 1, 1, 0, VECTOR)
+            first_matmul(a + 1, 1, 1, SCALAR)
+            quantise_xw(a, 1)
+
+        pass_0(last)
+        quantise_xw(last, 0)
+        first_matmul(last, 1, 0, SCALAR)
+        first_matmul(last, 1, 1, VECTOR)
+        first_matmul(last + 1, 1, 0, SCALAR)
+        quantise_xw(last, 1)
+        first_matmul(last + 1, 1, 1, VECTOR)
+        second_matmul(last - 2)
+        quantise_xw(last + 1, 1)
+        second_matmul(last - 1)
+        second_matmul(last)
+        finish(last - 2)
+        second_matmul(last + 1)
+        finish(last - 1)
+        finish(last)
+        finish(last + 1)

from contextlib import ExitStack

import concourse.mybir as mybir
from concourse.masks import make_identity

F32 = mybir.dt.float32
BF16 = mybir.dt.bfloat16
I32 = mybir.dt.int32
U32 = mybir.dt.uint32
U8 = mybir.dt.uint8
FP8X4 = mybir.dt.float8_e4m3fn_x4
ACT = mybir.ActivationFunctionType
ALU = mybir.AluOpType

P = 128
BATCHES, ROWS, FEATURES = 16, 256, 1024
PASS = 512
PASSES = FEATURES // PASS
GROUPS = 4
BLOCKS = ROWS // P
FLOPS = 2 * BATCHES * ROWS * FEATURES * FEATURES + 2 * BATCHES * ROWS * ROWS * FEATURES

VECTOR, SCALAR = "vector", "scalar"

QUANTISED_ALONE = ((14, 1), (15, 1))


def tile_columncorrelationhead_kernel(tc, column_embeddings, W, b, out):
    nc = tc.nc
    x_rows = column_embeddings.flatten_outer_dims().rearrange("(c p) d -> p c d", p=P)
    out_rows = out.flatten_outer_dims().rearrange("(c p) j -> p c j", p=P)
    w_view = W.rearrange("(a p e) c -> p a e c", a=4, p=P, e=2)

    with ExitStack() as ctx:
        ctx.enter_context(tc.manual_schedule())
        keep = ctx.enter_context(tc.tile_pool(name="keep", bufs=1))
        xg_pool = ctx.enter_context(tc.tile_pool(name="xg_pool", bufs=4))
        xwg_pool = ctx.enter_context(tc.tile_pool(name="xwg_pool", bufs=4))
        xwc_pool = ctx.enter_context(tc.tile_pool(name="xwc_pool", bufs=6))
        solo_pool = ctx.enter_context(tc.tile_pool(name="solo_pool", bufs=2))
        o_pool = ctx.enter_context(tc.tile_pool(name="o_pool", bufs=6))
        psum = ctx.enter_context(tc.psum_pool(name="psum", bufs=8))

        def copy(engine, dst, src):
            if engine == VECTOR:
                nc.vector.tensor_copy(out=dst, in_=src)
            else:
                nc.scalar.copy(out=dst, in_=src)

        zero_codes = keep.tile([P, PASS], U32, name="zero_codes", align_bytes=64)
        zero_scales = keep.tile([P, PASS], U8, name="zero_scales", align_bytes=64)
        zeros = keep.tile([P, 4 * PASS], BF16, name="zeros", align_bytes=64)
        nc.vector.memset(zeros[:].bitcast(I32), 0)
        nc.vector.quantize_mx(out=zero_codes[:].bitcast(FP8X4), scales=zero_scales[:], in_=zeros[:])
        ident = keep.tile([P, P], F32, name="ident")
        make_identity(nc, ident[:])
        diag_mask = keep.tile([P, P], F32, name="diag_mask")
        nc.vector.tensor_scalar(out=diag_mask[:], in0=ident[:], scalar1=2.0, scalar2=-1.0,
                                op0=ALU.mult, op1=ALU.add)
        b_bf16 = keep.tile([P, 1], BF16, name="b_bf16")
        nc.scalar.dma_start(out=b_bf16[:], in_=b.partition_broadcast(P))
        table_load = keep.tile([P, 1], F32, name="table_load")
        nc.scalar.activation(out=table_load[:], in_=ident[:, 0:1], func=ACT.Tanh)
        bias = keep.tile([P, 1], F32, name="bias")

        x_raw = [keep.tile([P, BLOCKS, FEATURES], BF16, name="x_raw%d" % n) for n in range(BATCHES)]
        x_codes = [keep.tile([P, PASSES, ROWS], U32, name="x_codes%d" % n, align_bytes=64)
                   for n in range(BATCHES)]
        x_scales = [keep.tile([P, PASSES, ROWS], U8, name="x_scales%d" % n, align_bytes=64)
                    for n in range(BATCHES)]
        w_raw, w_words, w_codes, w_scales = {}, {}, {}, {}
        for s in range(PASSES):
            for g in range(PASSES):
                w_raw[s, g] = keep.tile([P, 2, 2, PASS], BF16, name="w_raw%d%d" % (s, g))
                w_words[s, g] = keep.tile([P, 4 * PASS], BF16, name="w_words%d%d" % (s, g),
                                          align_bytes=64)
                w_codes[s, g] = keep.tile([P, PASS], U32, name="w_codes%d%d" % (s, g),
                                          align_bytes=64)
                w_scales[s, g] = keep.tile([P, PASS], U8, name="w_scales%d%d" % (s, g),
                                           align_bytes=64)
        live = {}

        def load_x(n):
            nc.sync.dma_start(out=x_raw[n][:], in_=x_rows[:, BLOCKS * n:BLOCKS * (n + 1), :])

        def load_w(s, g):
            for e in range(2):
                nc.sync.dma_start(out=w_raw[s, g][:, :, e, :],
                                  in_=w_view[:, 2 * g:2 * g + 2, e, s * PASS:(s + 1) * PASS])

        def warm_up(passes):
            scratch = psum.tile([P, PASS], F32, name="bank", tag="bank")
            for k in range(passes):
                nc.tensor.matmul_mx(out=scratch[:], lhsT=zero_codes[:, 0:P].bitcast(FP8X4),
                                    lhsT_scale=zero_scales[:, 0:P],
                                    rhs=zero_codes[:].bitcast(FP8X4), rhs_scale=zero_scales[:],
                                    start=True, stop=True)

        def transposes(n):
            pairs = x_raw[n][:].bitcast(F32)
            for g in range(PASSES):
                bank = psum.tile([P, 2, ROWS], F32, name="bank", tag="bank")
                for u in range(2):
                    for block in range(BLOCKS):
                        lo = (PASS // 2) * g + P * u
                        nc.tensor.transpose(bank[:, u, block * P:(block + 1) * P],
                                            pairs[:, block, lo:lo + P], ident[:])
                live["xT", n, g] = bank
            live["xg", n] = xg_pool.tile([P, PASSES, 4 * ROWS], BF16, name="xg", tag="xg",
                                         align_bytes=64)

        def copy_transposed(n, g, engine):
            pairs = live["xg", n][:].bitcast(F32)
            copy(engine, pairs[:, g, :].rearrange("p (i u) -> p i u", u=2),
                 live["xT", n, g][:].rearrange("p u i -> p i u"))

        def quantise_x(n):
            nc.vector.quantize_mx(out=x_codes[n][:].rearrange("p g i -> p (g i)").bitcast(FP8X4),
                                  scales=x_scales[n][:].rearrange("p g i -> p (g i)"),
                                  in_=live["xg", n][:].rearrange("p g c -> p (g c)"))

        def regroup_w(s, g, group, engine):
            v, f = divmod(group, 2)
            src = w_raw[s, g][:].rearrange("p u e c -> p (u e) c")
            src = src.rearrange("p t (v q f) -> p v f q t", v=2, q=P, f=2)[:, v, f]
            dst = w_words[s, g][:].rearrange("p (v f q t) -> p v f q t", v=2, f=2, q=P, t=4)[:, v, f]
            copy(engine, dst, src)

        def quantise_w(s, g, first_group, groups):
            words = slice(first_group * P, (first_group + groups) * P)
            nc.vector.quantize_mx(out=w_codes[s, g][:, words].bitcast(FP8X4),
                                  scales=w_scales[s, g][:, words],
                                  in_=w_words[s, g][:, 4 * first_group * P:4 * (first_group + groups) * P])

        def first_matmul_groups(n, s, block, groups):
            bank = live["xwT", n, s, block]
            rows = slice(block * P, (block + 1) * P)
            for t in groups:
                cols = slice(t * P, (t + 1) * P)
                for g in range(PASSES):
                    nc.tensor.matmul_mx(out=bank[:, cols],
                                        lhsT=w_codes[s, g][:, cols].bitcast(FP8X4),
                                        lhsT_scale=w_scales[s, g][:, cols],
                                        rhs=x_codes[n][:, g, rows].bitcast(FP8X4),
                                        rhs_scale=x_scales[n][:, g, rows],
                                        start=(g == 0), stop=(g == PASSES - 1))

        def first_matmul_open(n, s, block):
            live["xwT", n, s, block] = psum.tile([P, PASS], F32, name="bank", tag="bank")
            first_matmul_groups(n, s, block, (0, 1))

        def xw_place(n, s):
            if (n, s) in QUANTISED_ALONE:
                return (n, s), 0, 1
            return (n - n % 2, s), n % 2, 2

        def first_matmul_close(n, s, block, engine):
            first_matmul_groups(n, s, block, (2, 3))
            key, place, batches = xw_place(n, s)
            if ("xwg", key) not in live:
                if batches == 1:
                    live["xwg", key] = solo_pool.tile([P, ROWS, 4], BF16, name="xwg1", tag="xwg1",
                                                      align_bytes=64)
                else:
                    live["xwg", key] = xwg_pool.tile([P, 2 * ROWS, 4], BF16, name="xwg", tag="xwg",
                                                     align_bytes=64)
            lo = (BLOCKS * place + block) * P
            copy(engine, live["xwg", key][:, lo:lo + P, :],
                 live["xwT", n, s, block][:].rearrange("p (t i) -> p i t", t=GROUPS))

        def first_matmul(n, s, block, engine):
            first_matmul_open(n, s, block)
            first_matmul_close(n, s, block, engine)

        def quantise_xw(n, s):
            key, place, batches = xw_place(n, s)
            if batches == 1:
                codes = solo_pool.tile([P, ROWS], U32, name="xwc1", tag="xwc1", align_bytes=64)
                scales = solo_pool.tile([P, ROWS], U8, name="xws1", tag="xws1", align_bytes=64)
            else:
                codes = xwc_pool.tile([P, 2 * ROWS], U32, name="xwc", tag="xwc", align_bytes=64)
                scales = xwc_pool.tile([P, 2 * ROWS], U8, name="xws", tag="xws", align_bytes=64)
            nc.vector.quantize_mx(out=codes[:].bitcast(FP8X4), scales=scales[:],
                                  in_=live["xwg", key][:].rearrange("p i t -> p (i t)"))
            live["xwc", key] = (codes, scales)

        def second_matmul(n):
            result = o_pool.tile([P, BLOCKS, ROWS], F32, name="o", tag="o")
            live["o", n] = result
            bank = psum.tile([P, PASS], F32, name="bank", tag="bank")
            for block in range(BLOCKS):
                for s in range(PASSES):
                    key, place, batches = xw_place(n, s)
                    codes, scales = live["xwc", key]
                    rows = slice((BLOCKS * place + block) * P, (BLOCKS * place + block + 1) * P)
                    nc.tensor.matmul_mx(out=bank[:, block * ROWS:(block + 1) * ROWS],
                                        lhsT=codes[:, rows].bitcast(FP8X4),
                                        lhsT_scale=scales[:, rows],
                                        rhs=x_codes[n][:, s, :].bitcast(FP8X4),
                                        rhs_scale=x_scales[n][:, s, :],
                                        start=(s == 0), stop=(s == PASSES - 1))
            nc.scalar.activation(out=result[:], in_=bank[:].rearrange("p (r j) -> p r j", r=BLOCKS),
                                 func=ACT.Tanh, bias=bias[:, 0:1], scale=1.0)

        def finish(n):
            result = live["o", n]
            diagonal = result[:].rearrange("p r (a k) -> p (r a) k", k=P)[:, 0:4:3, :]
            nc.vector.tensor_tensor(out=diagonal, in0=diagonal,
                                    in1=diag_mask[:].unsqueeze(1).to_broadcast([P, BLOCKS, P]),
                                    op=ALU.max)
            nc.sync.dma_start(out=out_rows[:, BLOCKS * n:BLOCKS * (n + 1), :], in_=result[:])

        load_x(0)
        load_w(0, 0)
        load_w(0, 1)
        for n in range(1, 6):
            load_x(n)
        load_w(1, 0)
        load_w(1, 1)
        for n in range(6, BATCHES):
            load_x(n)

        warm_up(6)
        transposes(0)
        for group, engine in ((0, VECTOR), (1, VECTOR), (2, VECTOR), (3, SCALAR)):
            regroup_w(0, 0, group, engine)
        copy_transposed(0, 0, SCALAR)
        copy_transposed(0, 1, SCALAR)
        warm_up(5)
        quantise_w(0, 0, 0, 2)
        quantise_w(0, 0, 2, 2)
        regroup_w(0, 1, 0, SCALAR)
        regroup_w(0, 1, 1, VECTOR)
        quantise_x(0)
        transposes(1)
        quantise_w(0, 1, 0, 2)
        regroup_w(0, 1, 2, VECTOR)
        regroup_w(0, 1, 3, SCALAR)
        copy_transposed(1, 0, SCALAR)
        first_matmul_open(0, 0, 0)
        first_matmul_open(0, 0, 1)
        quantise_w(0, 1, 2, 2)
        nc.vector.tensor_copy(out=bias[:], in_=b_bf16[:])
        copy_transposed(1, 1, VECTOR)
        quantise_x(1)
        first_matmul_close(0, 0, 0, SCALAR)
        first_matmul_close(0, 0, 1, VECTOR)

        transposes(2)
        copy_transposed(2, 0, SCALAR)
        copy_transposed(2, 1, VECTOR)
        quantise_x(2)
        first_matmul(1, 0, 0, VECTOR)
        first_matmul(1, 0, 1, VECTOR)
        transposes(3)
        first_matmul(2, 0, 0, SCALAR)
        first_matmul(2, 0, 1, SCALAR)
        copy_transposed(3, 0, VECTOR)
        copy_transposed(3, 1, VECTOR)
        transposes(4)
        transposes(5)
        copy_transposed(4, 1, SCALAR)
        copy_transposed(5, 0, SCALAR)
        quantise_x(3)
        copy_transposed(5, 1, SCALAR)
        first_matmul(3, 0, 0, SCALAR)
        regroup_w(1, 0, 1, VECTOR)
        regroup_w(1, 0, 0, SCALAR)
        copy_transposed(4, 0, VECTOR)
        quantise_x(4)
        first_matmul(3, 0, 1, SCALAR)
        regroup_w(1, 0, 2, VECTOR)
        quantise_x(5)
        first_matmul(4, 0, 0, SCALAR)
        regroup_w(1, 0, 3, VECTOR)
        first_matmul(4, 0, 1, SCALAR)
        quantise_w(1, 0, 0, GROUPS)
        regroup_w(1, 1, 0, VECTOR)
        first_matmul(5, 0, 0, SCALAR)
        first_matmul(5, 0, 1, SCALAR)
        transposes(6)
        transposes(7)
        regroup_w(1, 1, 1, VECTOR)
        regroup_w(1, 1, 2, VECTOR)
        copy_transposed(6, 0, SCALAR)
        regroup_w(1, 1, 3, VECTOR)
        copy_transposed(7, 0, SCALAR)
        quantise_w(1, 1, 0, GROUPS)
        copy_transposed(7, 1, SCALAR)
        copy_transposed(6, 1, VECTOR)

        quantise_xw(0, 0)
        first_matmul(0, 1, 0, VECTOR)
        quantise_xw(2, 0)
        first_matmul(0, 1, 1, SCALAR)
        quantise_xw(4, 0)
        first_matmul(1, 1, 0, SCALAR)
        quantise_x(6)
        first_matmul(1, 1, 1, SCALAR)
        quantise_x(7)
        for n in (2, 3):
            for block in range(BLOCKS):
                first_matmul(n, 1, block, SCALAR)
        quantise_xw(0, 1)
        second_matmul(0)
        quantise_xw(2, 1)
        second_matmul(1)
        first_matmul(4, 1, 0, SCALAR)
        first_matmul(4, 1, 1, SCALAR)
        finish(0)
        first_matmul(5, 1, 0, VECTOR)
        first_matmul(5, 1, 1, SCALAR)
        second_matmul(2)
        quantise_xw(4, 1)
        finish(1)
        second_matmul(3)

        def pass_0(a):
            first_matmul(a, 0, 0, SCALAR)
            first_matmul(a, 0, 1, SCALAR)
            finish(a - 4)
            first_matmul(a + 1, 0, 0, VECTOR)
            finish(a - 3)
            first_matmul(a + 1, 0, 1, SCALAR)

        last = BATCHES - 2
        for a in range(6, last, 2):
            pass_0(a)
            second_matmul(a - 2)
            quantise_xw(a, 0)
            second_matmul(a - 1)
            transposes(a + 2)
            transposes(a + 3)
            copy_transposed(a + 2, 0, VECTOR)
            copy_transposed(a + 2, 1, VECTOR)
            copy_transposed(a + 3, 0, SCALAR)
            copy_transposed(a + 3, 1, VECTOR)
            quantise_x(a + 2)
            first_matmul(a, 1, 0, SCALAR)
            first_matmul(a, 1, 1, SCALAR)
            quantise_x(a + 3)
            first_matmul(a + 1, 1, 0, VECTOR)
            first_matmul(a + 1, 1, 1, SCALAR)
            quantise_xw(a, 1)

        pass_0(last)
        quantise_xw(last, 0)
        first_matmul(last, 1, 0, SCALAR)
        first_matmul(last, 1, 1, VECTOR)
        first_matmul(last + 1, 1, 0, SCALAR)
        quantise_xw(last, 1)
        first_matmul(last + 1, 1, 1, VECTOR)
        second_matmul(last - 2)
        quantise_xw(last + 1, 1)
        second_matmul(last - 1)
        second_matmul(last)
        finish(last - 2)
        second_matmul(last + 1)
        finish(last - 1)
        finish(last)
        finish(last + 1)
